import numpy as np
import ml_dtypes


def mxq(x, axis, fmt="e4m3"):
    dtype, down = {"e4m3": (ml_dtypes.float8_e4m3fn, 7), "e5m2": (ml_dtypes.float8_e5m2, 14)}[fmt]
    v = np.moveaxis(np.asarray(x, np.float32).astype(ml_dtypes.bfloat16).astype(np.float64), axis, -1)
    blocks = v.reshape(v.shape[:-1] + (-1, 32))
    amax = np.abs(blocks).max(-1, keepdims=True)
    byte = np.maximum(np.where(amax > 0, np.frexp(amax)[1] - 1 + 127, 0) - down, 1)
    scale = np.exp2(byte - 127.0)
    codes = (blocks / scale).astype(np.float32).astype(dtype).astype(np.float64)
    return np.moveaxis((codes * scale).reshape(v.shape), -1, axis)


WIDE = False


def mx_kscale(k):
    if not WIDE:
        return np.ones(k)
    levels = np.array([10, -10, 5, -5, 0])
    if k % 512:
        return np.exp2(np.random.permutation(np.resize(levels, k // 32))).repeat(32)
    a = np.empty((k // 512, 16))
    for p in range(k // 512):
        a[p, :8] = np.random.permutation(np.resize(levels, 8))
        for g in range(8):
            far = levels[np.abs(levels - a[p, g]) >= 10]
            a[p, g + 8] = far[np.random.randint(len(far))]
    return np.exp2(a.ravel()).repeat(32)


BF16 = ml_dtypes.bfloat16


def bf(x):
    return np.asarray(x, np.float32).astype(BF16)


def f64(x):
    return np.asarray(x).astype(np.float64)


B, S, D, P, PW, L = 2, 256, 1024, 4, 2, 2


def sigmoid(v):
    return 1.0 / (1.0 + np.exp(-v))


def draw0():
    n = np.random.standard_normal
    s = mx_kscale(D)
    return {"x": bf(n((B, S, D)) * s),
            "amp_w": bf(n((D, D)) / np.sqrt(D) / s[:, None]),
            "amp_b": bf(n(D) * 0.3),
            "ph_w": bf(n((D, D)) / np.sqrt(D) / s[:, None]),
            "ph_b": bf(n(D) * 0.3)}


def core(x, amp_w, amp_b, ph_w, ph_b):
    xq = mxq(f64(x), 2, "e4m3")
    amp = sigmoid((xq @ mxq(f64(amp_w), 0, "e4m3")) + f64(amp_b))
    ph = np.tanh((xq @ mxq(f64(ph_w), 0, "e4m3")) + f64(ph_b)) * np.pi
    return (np.cos(ph) + np.sin(ph)) * amp


def e4m3fn_bytes(y):
    return np.clip(np.asarray(y, np.float64), -448.0, 448.0).astype(np.float32).astype(ml_dtypes.float8_e4m3fn).view(np.uint8)


def e4m3fn_values(b):
    return np.asarray(b, np.uint8).view(ml_dtypes.float8_e4m3fn).astype(np.float64)


def setup_inputs():
    d = draw0()
    x0 = np.asarray(d['ph_w']).astype(np.float64)
    s = (np.max(np.abs(x0), axis=(1,), keepdims=True) / 448.0).astype(np.float32)
    out = {}
    for k, v in d.items():
        if k == 'ph_w':
            out['ph_w_bytes'] = e4m3fn_bytes(x0 / s.astype(np.float64))
            out['ph_w_scale'] = s
        else:
            out[k] = v
    return out


def reference(x, amp_w, amp_b, ph_w_bytes, ph_w_scale, ph_b):
    return core(x, amp_w, amp_b, e4m3fn_values(ph_w_bytes) * ph_w_scale.astype(np.float64), ph_b)

@@ -1,0 +1,261 @@
+import math
+from contextlib import ExitStack
+
+import concourse.mybir as mybir
+from concourse.masks import make_identity
+
+FLOPS = 2 * 2 * 512 * 1024 * 1024
+
+F32 = mybir.dt.float32
+BF16 = mybir.dt.bfloat16
+U32 = mybir.dt.uint32
+U8 = mybir.dt.uint8
+FP8 = mybir.dt.float8_e4m3fn
+FP8X4 = mybir.dt.float8_e4m3fn_x4
+ACT = mybir.ActivationFunctionType
+ALU = mybir.AluOpType
+
+P = 128
+TOK = 512
+K = 1024
+N = 1024
+G = 2
+T = 4
+NW = 256
+NCH = N // NW
+NT = N // P
+TPC = NW // P
+
+
+def tile_quantuminspiredneuralcore_pa_kernel(tc, x, amp_w, amp_b, ph_w_bytes, ph_w_scale, ph_b, out):
+    nc = tc.nc
+    xf = x.flatten_outer_dims()
+    of = out.flatten_outer_dims()
+    amp_v = amp_w.rearrange("(g p t) n -> g p t n", p=P, t=T)
+    phb_v = ph_w_bytes.rearrange("(g p t) n -> g p t n", p=P, t=T)
+    phs_v = ph_w_scale.rearrange("(g p t) o -> p g (t o)", p=P, t=T)
+    out_v = of.rearrange("(i p) n -> p i n", p=P)
+
+    with ExitStack() as ctx:
+        keep = ctx.enter_context(tc.tile_pool(name="keep", bufs=1))
+        work = ctx.enter_context(tc.tile_pool(name="work", bufs=3))
+        psum = ctx.enter_context(tc.psum_pool(name="psum", bufs=2))
+        ctx.enter_context(tc.manual_schedule())
+
+        warm_in = keep.tile([P, 1], F32, name="warm_in")
+        warm_out = keep.tile([P, 1], F32, name="warm_out")
+        brows = keep.tile([P, P], BF16, name="brows")
+        ident_f = keep.tile([P, P], F32, name="ident_f")
+        ident_b = keep.tile([P, P], BF16, name="ident_b")
+        ph_scale = keep.tile([P, G, T], F32, name="ph_scale")
+        bias = keep.tile([P, 2 * NT], F32, name="bias")
+        x_grouped = keep.tile([P, G, TOK, T], BF16, name="x_grouped", align_bytes=64)
+        x_codes = keep.tile([P, G, TOK], U32, name="x_codes", align_bytes=64)
+        x_scales = keep.tile([P, G, TOK], U8, name="x_scales", align_bytes=64)
+        xg_words = x_grouped[:].bitcast(F32)
+
+        ph_bytes = {}
+        raw = {}
+        x_sb = {}
+        xt = {}
+        grouped = {}
+        codes = {}
+        scales = {}
+        acc = {}
+        ep = {}
+
+        def load_bytes(c):
+            for g in range(G):
+                ph_bytes[(c, g)] = keep.tile([P, T, NW], U8, name="ph_bytes_%d_%d" % (c, g))
+                nc.sync.dma_start(out=ph_bytes[(c, g)][:], in_=phb_v[g][:, :, c * NW:(c + 1) * NW])
+
+        def load_amp(c):
+            raw[("a", c)] = keep.tile([P, G, T, NW], BF16, name="amp_raw_%d" % c)
+            for g in range(G):
+                nc.sync.dma_start(out=raw[("a", c)][:, g], in_=amp_v[g][:, :, c * NW:(c + 1) * NW])
+
+        def load_x(i):
+            x_sb[i] = keep.tile([P, K], BF16, name="x_sb_%d" % i)
+            nc.sync.dma_start(out=x_sb[i][:], in_=xf[i * P:(i + 1) * P, :])
+
+        def load_bias():
+            nc.sync.dma_start(out=brows[0:NT, :], in_=amp_b.rearrange("(j p) -> j p", p=P))
+            nc.sync.dma_start(out=brows[NT:2 * NT, :], in_=ph_b.rearrange("(j p) -> j p", p=P))
+
+        def bias_turn():
+            bT = psum.tile([P, P], BF16, name="bT", tag="tr", bufs=2)
+            nc.tensor.transpose(bT[:], brows[:], ident_b[:])
+            nc.vector.tensor_scalar(out=bias[:, 0:NT], in0=bT[:, 0:NT], scalar1=0.5, scalar2=None, op0=ALU.mult)
+            nc.vector.tensor_copy(out=bias[:, NT:2 * NT], in_=bT[:, NT:2 * NT])
+
+        def widen(c, g, on_scalar):
+            if g == 0:
+                raw[("p", c)] = keep.tile([P, G, T, NW], BF16, name="ph_wide_%d" % c)
+            for t in range(T):
+                src = ph_bytes[(c, g)][:, t, :].bitcast(FP8)
+                dst = raw[("p", c)][:, g, t, :]
+                if on_scalar:
+                    nc.scalar.activation(out=dst, in_=src, func=ACT.Copy, scale=ph_scale[:, g, t:t + 1])
+                else:
+                    nc.vector.tensor_scalar(out=dst, in0=src, scalar1=ph_scale[:, g, t:t + 1], scalar2=None, op0=ALU.mult)
+
+        def interleave(w, c):
+            grouped[(w, c)] = keep.tile([P, G, NW, T], BF16, name="grouped_%s_%d" % (w, c), align_bytes=64)
+            nc.vector.tensor_copy(out=grouped[(w, c)][:], in_=raw[(w, c)][:].rearrange("p g t n -> p g n t"))
+
+        def quantize(w, c):
+            codes[(w, c)] = keep.tile([P, G * NW], U32, name="codes_%s_%d" % (w, c), align_bytes=64)
+            scales[(w, c)] = keep.tile([P, G * NW], U8, name="scales_%s_%d" % (w, c), align_bytes=64)
+            nc.vector.quantize_mx(out=codes[(w, c)][:].bitcast(FP8X4), scales=scales[(w, c)][:],
+                                  in_=grouped[(w, c)][:].rearrange("p g n t -> p (g n t)"))
+
+        def x_turn(i):
+            xt[i] = psum.tile([P, G, 2, P], F32, name="xt_%d" % i, tag="acc", bufs=6)
+            words = x_sb[i][:].bitcast(F32)
+            for g in range(G):
+                for u in range(2):
+                    nc.tensor.transpose(xt[i][:, g, u, :], words[:, 256 * g + u:256 * (g + 1):2], ident_f[:])
+
+        def x_copy(i, on_scalar):
+            dst = xg_words[:, :, i * P:(i + 1) * P, :]
+            src = xt[i][:].rearrange("p g u r -> p g r u")
+            if on_scalar:
+                nc.scalar.copy(out=dst, in_=src)
+            else:
+                nc.vector.tensor_copy(out=dst, in_=src)
+
+        def x_quantize(g):
+            nc.vector.quantize_mx(out=x_codes[:, g, :].bitcast(FP8X4), scales=x_scales[:, g, :],
+                                  in_=x_grouped[:, g].rearrange("p r t -> p (r t)"))
+
+        def multiply(w, j):
+            c, h = divmod(j, TPC)
+            acc[(w, j)] = psum.tile([P, TOK], F32, name="acc_%s_%d" % (w, j), tag="acc", bufs=6)
+            for g in range(G):
+                cols = slice(g * NW + h * P, g * NW + (h + 1) * P)
+                nc.tensor.matmul_mx(out=acc[(w, j)][:],
+                                    lhsT=codes[(w, c)][:, cols].bitcast(FP8X4), lhsT_scale=scales[(w, c)][:, cols],
+                                    rhs=x_codes[:, g, :].bitcast(FP8X4), rhs_scale=x_scales[:, g, :],
+                                    start=(g == 0), stop=(g == G - 1))
+
+        def new(kind, j):
+            ep[(kind, j)] = work.tile([P, TOK], F32, name="%s_%d" % (kind, j), tag=kind)
+            return ep[(kind, j)]
+
+        def s_tp(j):
+            nc.scalar.activation(out=new("tp", j)[:], in_=acc[("p", j)][:], func=ACT.Tanh, bias=bias[:, NT + j:NT + j + 1], scale=1.0)
+
+        def s_th(j):
+            nc.scalar.activation(out=new("th", j)[:], in_=acc[("a", j)][:], func=ACT.Tanh, bias=bias[:, j:j + 1], scale=0.5)
+
+        def s_ab(j):
+            nc.scalar.activation(out=new("ab", j)[:], in_=ep[("tp", j)][:], func=ACT.Abs, bias=-0.25, scale=1.0)
+
+        def s_sn(j):
+            nc.scalar.activation(out=new("sn", j)[:], in_=ep[("ab", j)][:], func=ACT.Sin, bias=math.pi / 2, scale=-math.pi)
+
+        def product(j, lo=0, hi=TOK):
+            if lo == 0:
+                new("prod", j)
+            nc.vector.scalar_tensor_tensor(out=ep[("prod", j)][:, lo:hi], in0=ep[("th", j)][:, lo:hi], scalar=1.0,
+                                           in1=ep[("sn", j)][:, lo:hi], op0=ALU.add, op1=ALU.mult)
+
+        def turn_back(j, lo=0, hi=TOK):
+            ni = (hi - lo) // P
+            ep[("oT", j, lo)] = psum.tile([P, ni, P], F32, name="oT_%d_%d" % (j, lo), tag="tr", bufs=2)
+            for i in range(ni):
+                nc.tensor.transpose(ep[("oT", j, lo)][:, i, :], ep[("prod", j)][:, lo + i * P:lo + (i + 1) * P], ident_f[:])
+
+        def copy_out(j, on_scalar, lo=0, hi=TOK):
+            ni = (hi - lo) // P
+            i0 = lo // P
+            o_sb = work.tile([P, ni, P], F32, name="o_sb_%d_%d" % (j, lo), tag="o_sb", bufs=4)
+            if on_scalar:
+                nc.scalar.activation(out=o_sb[:], in_=ep[("oT", j, lo)][:], func=ACT.Copy, scale=math.sqrt(0.5))
+            else:
+                nc.vector.tensor_scalar(out=o_sb[:], in0=ep[("oT", j, lo)][:], scalar1=math.sqrt(0.5), scalar2=None, op0=ALU.mult)
+            nc.sync.dma_start(out=out_v[:, i0:i0 + ni, j * P:(j + 1) * P], in_=o_sb[:])
+
+        nc.vector.memset(warm_in[:], 0.0)
+        nc.vector.memset(brows[:], 0.0)
+        nc.scalar.activation(out=warm_out[:], in_=warm_in[:], func=ACT.Silu)
+        make_identity(nc, ident_b[:])
+        make_identity(nc, ident_f[:])
+
+        nc.sync.dma_start(out=ph_scale[:], in_=phs_v)
+        load_bytes(0)
+        load_bias()
+        for i in range(4):
+            load_x(i)
+        load_amp(0)
+        load_bytes(1)
+        load_amp(1)
+        load_bytes(2)
+        load_amp(2)
+        load_bytes(3)
+        load_amp(3)
+
+        widen(0, 0, False)
+        widen(0, 1, True)
+        bias_turn()
+        for i in range(4):
+            x_turn(i)
+            x_copy(i, True)
+        interleave("p", 0)
+        widen(1, 0, True)
+        widen(1, 1, True)
+        quantize("p", 0)
+        x_quantize(0)
+        x_quantize(1)
+        multiply("p", 0)
+        multiply("p", 1)
+        interleave("a", 0)
+        quantize("a", 0)
+        multiply("a", 0)
+        multiply("a", 1)
+
+        V_WIDEN = (2, 3)
+        S_OUT = (0, 1, 2, 3)
+        for c in range(NCH):
+            a, b = 2 * c, 2 * c + 1
+            last = c == NCH - 1
+            if not last:
+                interleave("p", c + 1)
+            s_tp(a)
+            s_tp(b)
+            if c > 0:
+                product(b - 2)
+                turn_back(b - 2)
+            if not last:
+                quantize("p", c + 1)
+                multiply("p", a + 2)
+                multiply("p", b + 2)
+            s_ab(a)
+            s_th(a)
+            s_sn(a)
+            if not last:
+                interleave("a", c + 1)
+            if c > 0:
+                copy_out(a - 2, a - 2 in S_OUT)
+            s_ab(b)
+            s_th(b)
+            if c > 0:
+                copy_out(b - 2, b - 2 in S_OUT)
+            s_sn(b)
+            product(a)
+            turn_back(a)
+            if not last:
+                quantize("a", c + 1)
+                multiply("a", a + 2)
+                multiply("a", b + 2)
+            if c + 2 in V_WIDEN:
+                widen(c + 2, 0, False)
+                widen(c + 2, 1, False)
+        copy_out(NT - 2, False)
+        j = NT - 1
+        product(j, 0, 256)
+        turn_back(j, 0, 256)
+        product(j, 256, 512)
+        turn_back(j, 256, 512)
+        copy_out(j, False, 0, 256)
+        copy_out(j, True, 256, 512)

@@ -70,9 +70,9 @@ def tile_quantuminspiredneuralcore_pa_kernel(tc, x, amp_w, amp_b, ph_w_bytes, ph
                 nc.sync.dma_start(out=ph_bytes[(c, g)][:], in_=phb_v[g][:, :, c * NW:(c + 1) * NW])
 
         def load_amp(c):
-            raw[("a", c)] = keep.tile([P, G, T, NW], BF16, name="amp_raw_%d" % c)
+            raw[("a", c)] = keep.tile([P, T, G, NW], BF16, name="amp_raw_%d" % c)
             for g in range(G):
-                nc.sync.dma_start(out=raw[("a", c)][:, g], in_=amp_v[g][:, :, c * NW:(c + 1) * NW])
+                nc.sync.dma_start(out=raw[("a", c)][:, :, g, :], in_=amp_v[g][:, :, c * NW:(c + 1) * NW])
 
         def load_x(i):
             x_sb[i] = keep.tile([P, K], BF16, name="x_sb_%d" % i)
@@ -90,24 +90,25 @@ def tile_quantuminspiredneuralcore_pa_kernel(tc, x, amp_w, amp_b, ph_w_bytes, ph
 
         def widen(c, g, on_scalar):
             if g == 0:
-                raw[("p", c)] = keep.tile([P, G, T, NW], BF16, name="ph_wide_%d" % c)
+                raw[("p", c)] = keep.tile([P, T, G, NW], BF16, name="ph_wide_%d" % c)
             for t in range(T):
                 src = ph_bytes[(c, g)][:, t, :].bitcast(FP8)
-                dst = raw[("p", c)][:, g, t, :]
+                dst = raw[("p", c)][:, t, g, :]
                 if on_scalar:
                     nc.scalar.activation(out=dst, in_=src, func=ACT.Copy, scale=ph_scale[:, g, t:t + 1])
                 else:
                     nc.vector.tensor_scalar(out=dst, in0=src, scalar1=ph_scale[:, g, t:t + 1], scalar2=None, op0=ALU.mult)
 
         def interleave(w, c):
-            grouped[(w, c)] = keep.tile([P, G, NW, T], BF16, name="grouped_%s_%d" % (w, c), align_bytes=64)
-            nc.vector.tensor_copy(out=grouped[(w, c)][:], in_=raw[(w, c)][:].rearrange("p g t n -> p g n t"))
+            grouped[(w, c)] = keep.tile([P, G * NW, T], BF16, name="grouped_%s_%d" % (w, c), align_bytes=64)
+            nc.vector.tensor_copy(out=grouped[(w, c)][:].rearrange("p (c i) t -> p c t i", i=4),
+                                  in_=raw[(w, c)][:].rearrange("p t g n -> p t (g n)").rearrange("p t (c i) -> p c t i", i=4))
 
         def quantize(w, c):
             codes[(w, c)] = keep.tile([P, G * NW], U32, name="codes_%s_%d" % (w, c), align_bytes=64)
             scales[(w, c)] = keep.tile([P, G * NW], U8, name="scales_%s_%d" % (w, c), align_bytes=64)
             nc.vector.quantize_mx(out=codes[(w, c)][:].bitcast(FP8X4), scales=scales[(w, c)][:],
-                                  in_=grouped[(w, c)][:].rearrange("p g n t -> p (g n t)"))
+                                  in_=grouped[(w, c)][:].rearrange("p m t -> p (m t)"))
 
         def x_turn(i):
             xt[i] = psum.tile([P, G, 2, P], F32, name="xt_%d" % i, tag="acc", bufs=6)

@@ -64,10 +64,10 @@ def tile_quantuminspiredneuralcore_pa_kernel(tc, x, amp_w, amp_b, ph_w_bytes, ph
         acc = {}
         ep = {}
 
-        def load_bytes(c):
+        def load_bytes(h):
             for g in range(G):
-                ph_bytes[(c, g)] = keep.tile([P, T, NW], U8, name="ph_bytes_%d_%d" % (c, g))
-                nc.sync.dma_start(out=ph_bytes[(c, g)][:], in_=phb_v[g][:, :, c * NW:(c + 1) * NW])
+                ph_bytes[(h, g)] = keep.tile([P, T, 2 * NW], U8, name="ph_bytes_%d_%d" % (h, g))
+                nc.sync.dma_start(out=ph_bytes[(h, g)][:], in_=phb_v[g][:, :, h * 2 * NW:(h + 1) * 2 * NW])
 
         def load_amp(c):
             raw[("a", c)] = keep.tile([P, T, G, NW], BF16, name="amp_raw_%d" % c)
@@ -88,11 +88,11 @@ def tile_quantuminspiredneuralcore_pa_kernel(tc, x, amp_w, amp_b, ph_w_bytes, ph
             nc.vector.tensor_scalar(out=bias[:, 0:NT], in0=bT[:, 0:NT], scalar1=0.5, scalar2=None, op0=ALU.mult)
             nc.vector.tensor_copy(out=bias[:, NT:2 * NT], in_=bT[:, NT:2 * NT])
 
-        def widen(c, g, on_scalar):
-            if g == 0:
+        def widen(c, g, on_scalar, planes=(0, 1, 2, 3)):
+            if ("p", c) not in raw:
                 raw[("p", c)] = keep.tile([P, T, G, NW], BF16, name="ph_wide_%d" % c)
-            for t in range(T):
-                src = ph_bytes[(c, g)][:, t, :].bitcast(FP8)
+            for t in planes:
+                src = ph_bytes[(c // 2, g)][:, t, (c % 2) * NW:(c % 2 + 1) * NW].bitcast(FP8)
                 dst = raw[("p", c)][:, t, g, :]
                 if on_scalar:
                     nc.scalar.activation(out=dst, in_=src, func=ACT.Copy, scale=ph_scale[:, g, t:t + 1])
@@ -117,9 +117,9 @@ def tile_quantuminspiredneuralcore_pa_kernel(tc, x, amp_w, amp_b, ph_w_bytes, ph
                 for u in range(2):
                     nc.tensor.transpose(xt[i][:, g, u, :], words[:, 256 * g + u:256 * (g + 1):2], ident_f[:])
 
-        def x_copy(i, on_scalar):
-            dst = xg_words[:, :, i * P:(i + 1) * P, :]
-            src = xt[i][:].rearrange("p g u r -> p g r u")
+        def x_copy(i, on_scalar, g0=0, g1=G):
+            dst = xg_words[:, g0:g1, i * P:(i + 1) * P, :]
+            src = xt[i][:, g0:g1].rearrange("p g u r -> p g r u")
             if on_scalar:
                 nc.scalar.copy(out=dst, in_=src)
             else:
@@ -152,8 +152,10 @@ def tile_quantuminspiredneuralcore_pa_kernel(tc, x, amp_w, amp_b, ph_w_bytes, ph
         def s_ab(j):
             nc.scalar.activation(out=new("ab", j)[:], in_=ep[("tp", j)][:], func=ACT.Abs, bias=-0.25, scale=1.0)
 
-        def s_sn(j):
-            nc.scalar.activation(out=new("sn", j)[:], in_=ep[("ab", j)][:], func=ACT.Sin, bias=math.pi / 2, scale=-math.pi)
+        def s_sn(j, lo=0, hi=TOK):
+            if lo == 0:
+                new("sn", j)
+            nc.scalar.activation(out=ep[("sn", j)][:, lo:hi], in_=ep[("ab", j)][:, lo:hi], func=ACT.Sin, bias=math.pi / 2, scale=-math.pi)
 
         def product(j, lo=0, hi=TOK):
             if lo == 0:
@@ -161,9 +163,12 @@ def tile_quantuminspiredneuralcore_pa_kernel(tc, x, amp_w, amp_b, ph_w_bytes, ph
             nc.vector.scalar_tensor_tensor(out=ep[("prod", j)][:, lo:hi], in0=ep[("th", j)][:, lo:hi], scalar=1.0,
                                            in1=ep[("sn", j)][:, lo:hi], op0=ALU.add, op1=ALU.mult)
 
-        def turn_back(j, lo=0, hi=TOK):
+        def turn_back(j, lo=0, hi=TOK, spare=False):
             ni = (hi - lo) // P
-            ep[("oT", j, lo)] = psum.tile([P, ni, P], F32, name="oT_%d_%d" % (j, lo), tag="tr", bufs=2)
+            if spare:
+                ep[("oT", j, lo)] = psum.tile([P, ni, P], F32, name="oT_%d_%d" % (j, lo), tag="acc", bufs=6)
+            else:
+                ep[("oT", j, lo)] = psum.tile([P, ni, P], F32, name="oT_%d_%d" % (j, lo), tag="tr", bufs=2)
             for i in range(ni):
                 nc.tensor.transpose(ep[("oT", j, lo)][:, i, :], ep[("prod", j)][:, lo + i * P:lo + (i + 1) * P], ident_f[:])
 
@@ -191,26 +196,30 @@ def tile_quantuminspiredneuralcore_pa_kernel(tc, x, amp_w, amp_b, ph_w_bytes, ph
         load_amp(0)
         load_bytes(1)
         load_amp(1)
-        load_bytes(2)
         load_amp(2)
-        load_bytes(3)
         load_amp(3)
 
         widen(0, 0, False)
-        widen(0, 1, True)
+        widen(0, 1, False)
+        widen(1, 0, True)
+        widen(1, 1, True, (0, 1))
+        interleave("p", 0)
         bias_turn()
-        for i in range(4):
+        for i in range(3):
             x_turn(i)
             x_copy(i, True)
-        interleave("p", 0)
-        widen(1, 0, True)
-        widen(1, 1, True)
+        x_turn(3)
+        x_copy(3, True, 0, 1)
+        x_copy(3, True, 1, 2)
+        widen(1, 1, True, (2, 3))
+        widen(2, 0, True)
         quantize("p", 0)
         x_quantize(0)
         x_quantize(1)
         multiply("p", 0)
         multiply("p", 1)
         interleave("a", 0)
+        interleave("p", 1)
         quantize("a", 0)
         multiply("a", 0)
         multiply("a", 1)
@@ -220,7 +229,7 @@ def tile_quantuminspiredneuralcore_pa_kernel(tc, x, amp_w, amp_b, ph_w_bytes, ph
         for c in range(NCH):
             a, b = 2 * c, 2 * c + 1
             last = c == NCH - 1
-            if not last:
+            if not last and c > 0:
                 interleave("p", c + 1)
             s_tp(a)
             s_tp(b)
@@ -232,17 +241,18 @@ def tile_quantuminspiredneuralcore_pa_kernel(tc, x, amp_w, amp_b, ph_w_bytes, ph
                 multiply("p", a + 2)
                 multiply("p", b + 2)
             s_ab(a)
-            s_th(a)
+            s_ab(b)
             s_sn(a)
             if not last:
                 interleave("a", c + 1)
             if c > 0:
                 copy_out(a - 2, a - 2 in S_OUT)
-            s_ab(b)
-            s_th(b)
+            s_th(a)
+            if not last:
+                s_sn(b)
             if c > 0:
                 copy_out(b - 2, b - 2 in S_OUT)
-            s_sn(b)
+            s_th(b)
             product(a)
             turn_back(a)
             if not last:
@@ -250,13 +260,16 @@ def tile_quantuminspiredneuralcore_pa_kernel(tc, x, amp_w, amp_b, ph_w_bytes, ph
                 multiply("a", a + 2)
                 multiply("a", b + 2)
             if c + 2 in V_WIDEN:
-                widen(c + 2, 0, False)
+                if c + 2 > 2:
+                    widen(c + 2, 0, False)
                 widen(c + 2, 1, False)
-        copy_out(NT - 2, False)
         j = NT - 1
+        s_sn(j, 0, 256)
+        s_sn(j, 256, 512)
         product(j, 0, 256)
-        turn_back(j, 0, 256)
+        turn_back(j, 0, 256, True)
         product(j, 256, 512)
-        turn_back(j, 256, 512)
+        turn_back(j, 256, 512, True)
+        copy_out(NT - 2, True)
         copy_out(j, False, 0, 256)
         copy_out(j, True, 256, 512)

@@ -25,6 +25,8 @@ NW = 256
 NCH = N // NW
 NT = N // P
 TPC = NW // P
+NI = TOK // P
+HALF = TOK // 2
 
 
 def tile_quantuminspiredneuralcore_pa_kernel(tc, x, amp_w, amp_b, ph_w_bytes, ph_w_scale, ph_b, out):
@@ -47,6 +49,7 @@ def tile_quantuminspiredneuralcore_pa_kernel(tc, x, amp_w, amp_b, ph_w_bytes, ph
         brows = keep.tile([P, P], BF16, name="brows")
         ident_f = keep.tile([P, P], F32, name="ident_f")
         ident_b = keep.tile([P, P], BF16, name="ident_b")
+        ones_b = keep.tile([P, TOK], BF16, name="ones_b")
         ph_scale = keep.tile([P, G, T], F32, name="ph_scale")
         bias = keep.tile([P, 2 * NT], F32, name="bias")
         x_grouped = keep.tile([P, G, TOK, T], BF16, name="x_grouped", align_bytes=64)
@@ -64,10 +67,12 @@ def tile_quantuminspiredneuralcore_pa_kernel(tc, x, amp_w, amp_b, ph_w_bytes, ph
         acc = {}
         ep = {}
 
-        def load_bytes(h):
+        def load_bytes(c0, c1):
             for g in range(G):
-                ph_bytes[(h, g)] = keep.tile([P, T, 2 * NW], U8, name="ph_bytes_%d_%d" % (h, g))
-                nc.sync.dma_start(out=ph_bytes[(h, g)][:], in_=phb_v[g][:, :, h * 2 * NW:(h + 1) * 2 * NW])
+                both = keep.tile([P, T, (c1 - c0) * NW], U8, name="ph_bytes_%d_%d" % (c0, g))
+                nc.sync.dma_start(out=both[:], in_=phb_v[g][:, :, c0 * NW:c1 * NW])
+                for c in range(c0, c1):
+                    ph_bytes[(c, g)] = both[:, :, (c - c0) * NW:(c - c0 + 1) * NW]
 
         def load_amp(c):
             raw[("a", c)] = keep.tile([P, T, G, NW], BF16, name="amp_raw_%d" % c)
@@ -82,56 +87,59 @@ def tile_quantuminspiredneuralcore_pa_kernel(tc, x, amp_w, amp_b, ph_w_bytes, ph
             nc.sync.dma_start(out=brows[0:NT, :], in_=amp_b.rearrange("(j p) -> j p", p=P))
             nc.sync.dma_start(out=brows[NT:2 * NT, :], in_=ph_b.rearrange("(j p) -> j p", p=P))
 
-        def bias_turn():
-            bT = psum.tile([P, P], BF16, name="bT", tag="tr", bufs=2)
-            nc.tensor.transpose(bT[:], brows[:], ident_b[:])
-            nc.vector.tensor_scalar(out=bias[:, 0:NT], in0=bT[:, 0:NT], scalar1=0.5, scalar2=None, op0=ALU.mult)
-            nc.vector.tensor_copy(out=bias[:, NT:2 * NT], in_=bT[:, NT:2 * NT])
+        def bias_turn(on_scalar):
+            ep["bT"] = psum.tile([P, P], BF16, name="bT", tag="tpT")
+            nc.tensor.transpose(ep["bT"][:], brows[:], ident_b[:])
 
-        def widen(c, g, on_scalar, planes=(0, 1, 2, 3)):
+        def bias_copy(on_scalar):
+            nc.vector.tensor_scalar(out=bias[:, 0:NT], in0=ep["bT"][:, 0:NT], scalar1=0.5, scalar2=None, op0=ALU.mult)
+            nc.vector.tensor_copy(out=bias[:, NT:2 * NT], in_=ep["bT"][:, NT:2 * NT])
+
+        def widen(on_scalar, c, k):
             if ("p", c) not in raw:
                 raw[("p", c)] = keep.tile([P, T, G, NW], BF16, name="ph_wide_%d" % c)
-            for t in planes:
-                src = ph_bytes[(c // 2, g)][:, t, (c % 2) * NW:(c % 2 + 1) * NW].bitcast(FP8)
-                dst = raw[("p", c)][:, t, g, :]
-                if on_scalar:
-                    nc.scalar.activation(out=dst, in_=src, func=ACT.Copy, scale=ph_scale[:, g, t:t + 1])
-                else:
-                    nc.vector.tensor_scalar(out=dst, in0=src, scalar1=ph_scale[:, g, t:t + 1], scalar2=None, op0=ALU.mult)
+            g, t = divmod(k, T)
+            src = ph_bytes[(c, g)][:, t, :].bitcast(FP8)
+            dst = raw[("p", c)][:, t, g, :]
+            if on_scalar:
+                nc.scalar.activation(out=dst, in_=src, func=ACT.Copy, scale=ph_scale[:, g, t:t + 1])
+            else:
+                nc.vector.tensor_scalar(out=dst, in0=src, scalar1=ph_scale[:, g, t:t + 1], scalar2=None, op0=ALU.mult)
 
-        def interleave(w, c):
+        def interleave(on_scalar, w, c):
             grouped[(w, c)] = keep.tile([P, G * NW, T], BF16, name="grouped_%s_%d" % (w, c), align_bytes=64)
             nc.vector.tensor_copy(out=grouped[(w, c)][:].rearrange("p (c i) t -> p c t i", i=4),
                                   in_=raw[(w, c)][:].rearrange("p t g n -> p t (g n)").rearrange("p t (c i) -> p c t i", i=4))
 
-        def quantize(w, c):
+        def quantize(on_scalar, w, c):
             codes[(w, c)] = keep.tile([P, G * NW], U32, name="codes_%s_%d" % (w, c), align_bytes=64)
             scales[(w, c)] = keep.tile([P, G * NW], U8, name="scales_%s_%d" % (w, c), align_bytes=64)
             nc.vector.quantize_mx(out=codes[(w, c)][:].bitcast(FP8X4), scales=scales[(w, c)][:],
                                   in_=grouped[(w, c)][:].rearrange("p m t -> p (m t)"))
 
-        def x_turn(i):
-            xt[i] = psum.tile([P, G, 2, P], F32, name="xt_%d" % i, tag="acc", bufs=6)
+        def x_turn(on_scalar, i):
+            xt[i] = psum.tile([P, G, 2, P], F32, name="xt_%d" % i, tag=("zp", "za")[i % 2])
             words = x_sb[i][:].bitcast(F32)
             for g in range(G):
                 for u in range(2):
                     nc.tensor.transpose(xt[i][:, g, u, :], words[:, 256 * g + u:256 * (g + 1):2], ident_f[:])
 
-        def x_copy(i, on_scalar, g0=0, g1=G):
-            dst = xg_words[:, g0:g1, i * P:(i + 1) * P, :]
-            src = xt[i][:, g0:g1].rearrange("p g u r -> p g r u")
+        def x_copy(on_scalar, i):
+            dst = xg_words[:, :, i * P:(i + 1) * P, :]
+            src = xt[i][:].rearrange("p g u r -> p g r u")
             if on_scalar:
                 nc.scalar.copy(out=dst, in_=src)
             else:
                 nc.vector.tensor_copy(out=dst, in_=src)
 
-        def x_quantize(g):
-            nc.vector.quantize_mx(out=x_codes[:, g, :].bitcast(FP8X4), scales=x_scales[:, g, :],
-                                  in_=x_grouped[:, g].rearrange("p r t -> p (r t)"))
+        def x_quantize(on_scalar, h, g):
+            lo, hi = h * HALF, (h + 1) * HALF
+            nc.vector.quantize_mx(out=x_codes[:, g, lo:hi].bitcast(FP8X4), scales=x_scales[:, g, lo:hi],
+                                  in_=x_grouped[:, g, lo:hi].rearrange("p r t -> p (r t)"))
 
-        def multiply(w, j):
+        def multiply(on_scalar, w, j):
             c, h = divmod(j, TPC)
-            acc[(w, j)] = psum.tile([P, TOK], F32, name="acc_%s_%d" % (w, j), tag="acc", bufs=6)
+            acc[(w, j)] = psum.tile([P, TOK], F32, name="acc_%s_%d" % (w, j), tag="z" + w)
             for g in range(G):
                 cols = slice(g * NW + h * P, g * NW + (h + 1) * P)
                 nc.tensor.matmul_mx(out=acc[(w, j)][:],
@@ -143,133 +151,129 @@ def tile_quantuminspiredneuralcore_pa_kernel(tc, x, amp_w, amp_b, ph_w_bytes, ph
             ep[(kind, j)] = work.tile([P, TOK], F32, name="%s_%d" % (kind, j), tag=kind)
             return ep[(kind, j)]
 
-        def s_tp(j):
+        def tanh_ph(on_scalar, j):
             nc.scalar.activation(out=new("tp", j)[:], in_=acc[("p", j)][:], func=ACT.Tanh, bias=bias[:, NT + j:NT + j + 1], scale=1.0)
 
-        def s_th(j):
+        def tanh_amp(on_scalar, j):
             nc.scalar.activation(out=new("th", j)[:], in_=acc[("a", j)][:], func=ACT.Tanh, bias=bias[:, j:j + 1], scale=0.5)
 
-        def s_ab(j):
-            nc.scalar.activation(out=new("ab", j)[:], in_=ep[("tp", j)][:], func=ACT.Abs, bias=-0.25, scale=1.0)
+        def turn_ph(on_scalar, j):
+            ep[("tpT", j)] = psum.tile([P, TOK], F32, name="tpT_%d" % j, tag="tpT")
+            for i in range(NI):
+                nc.tensor.transpose(ep[("tpT", j)][:, i * P:(i + 1) * P], ep[("tp", j)][:, i * P:(i + 1) * P], ident_f[:])
 
-        def s_sn(j, lo=0, hi=TOK):
+        def turn_amp(on_scalar, j):
+            ep[("thT", j)] = psum.tile([P, TOK], F32, name="thT_%d" % j, tag="thT")
+            nc.tensor.matmul(out=ep[("thT", j)][:], lhsT=ident_b[:], rhs=ones_b[:], start=True, stop=False)
+            for i in range(NI):
+                nc.tensor.matmul(out=ep[("thT", j)][:, i * P:(i + 1) * P], lhsT=ep[("th", j)][:, i * P:(i + 1) * P], rhs=ident_f[:],
+                                 is_transpose=True, start=False, stop=(i == NI - 1))
+
+        def fold(on_scalar, j):
+            nc.scalar.activation(out=new("ab", j)[:], in_=ep[("tpT", j)][:], func=ACT.Abs, bias=-0.25, scale=1.0)
+
+        def sine(on_scalar, j, lo=0, hi=TOK):
             if lo == 0:
                 new("sn", j)
             nc.scalar.activation(out=ep[("sn", j)][:, lo:hi], in_=ep[("ab", j)][:, lo:hi], func=ACT.Sin, bias=math.pi / 2, scale=-math.pi)
 
-        def product(j, lo=0, hi=TOK):
-            if lo == 0:
-                new("prod", j)
-            nc.vector.scalar_tensor_tensor(out=ep[("prod", j)][:, lo:hi], in0=ep[("th", j)][:, lo:hi], scalar=1.0,
-                                           in1=ep[("sn", j)][:, lo:hi], op0=ALU.add, op1=ALU.mult)
+        def product(on_scalar, j, lo=0, hi=TOK):
+            o_sb = work.tile([P, hi - lo], F32, name="o_sb_%d_%d" % (j, lo), tag="o_sb", bufs=4)
+            nc.vector.scalar_tensor_tensor(out=o_sb[:], in0=ep[("sn", j)][:, lo:hi], scalar=math.sqrt(0.5),
+                                           in1=ep[("thT", j)][:, lo:hi], op0=ALU.mult, op1=ALU.mult)
+            nc.sync.dma_start(out=out_v[:, lo // P:hi // P, j * P:(j + 1) * P], in_=o_sb[:].rearrange("p (i n) -> p i n", n=P))
 
-        def turn_back(j, lo=0, hi=TOK, spare=False):
-            ni = (hi - lo) // P
-            if spare:
-                ep[("oT", j, lo)] = psum.tile([P, ni, P], F32, name="oT_%d_%d" % (j, lo), tag="acc", bufs=6)
-            else:
-                ep[("oT", j, lo)] = psum.tile([P, ni, P], F32, name="oT_%d_%d" % (j, lo), tag="tr", bufs=2)
-            for i in range(ni):
-                nc.tensor.transpose(ep[("oT", j, lo)][:, i, :], ep[("prod", j)][:, lo + i * P:lo + (i + 1) * P], ident_f[:])
+        steps = {"bT": bias_turn, "bias": bias_copy, "widen": widen, "il": interleave, "q": quantize, "xT": x_turn, "xc": x_copy,
+                 "xq": x_quantize, "mx": multiply, "tp": tanh_ph, "th": tanh_amp, "tpT": turn_ph, "thT": turn_amp, "ab": fold,
+                 "sn": sine, "pr": product}
 
-        def copy_out(j, on_scalar, lo=0, hi=TOK):
-            ni = (hi - lo) // P
-            i0 = lo // P
-            o_sb = work.tile([P, ni, P], F32, name="o_sb_%d_%d" % (j, lo), tag="o_sb", bufs=4)
-            if on_scalar:
-                nc.scalar.activation(out=o_sb[:], in_=ep[("oT", j, lo)][:], func=ACT.Copy, scale=math.sqrt(0.5))
-            else:
-                nc.vector.tensor_scalar(out=o_sb[:], in0=ep[("oT", j, lo)][:], scalar1=math.sqrt(0.5), scalar2=None, op0=ALU.mult)
-            nc.sync.dma_start(out=out_v[:, i0:i0 + ni, j * P:(j + 1) * P], in_=o_sb[:])
+        def needs(s):
+            kind = s[0]
+            j = s[2] if kind in ("il", "q", "mx") else s[-1] if len(s) == 2 else s[1] if len(s) > 1 else 0
+            x_done = [("xq", h, g) for h in range(2) for g in range(G)]
+            if kind == "il":
+                return [("widen", j, k) for k in range(G * T)] if s[1] == "p" else []
+            if kind == "q":
+                return [("il", s[1], j)]
+            if kind == "xT":
+                return [("xc", j - 2)] if j >= 2 else []
+            if kind == "xc":
+                return [("xT", j)]
+            if kind == "xq":
+                return [("xc", 2 * s[1]), ("xc", 2 * s[1] + 1)]
+            if kind == "bias":
+                return [("bT",)]
+            if kind == "mx":
+                return [("q", s[1], j // TPC)] + x_done + ([({"p": "tp", "a": "th"}[s[1]], j - 2)] if j >= 2 else [])
+            if kind == "tp":
+                return [("mx", "p", j), ("bias",)] + ([("tpT", j - 3)] if j >= 3 else [])
+            if kind == "th":
+                return [("mx", "a", j), ("bias",)] + ([("thT", j - 3)] if j >= 3 else [])
+            if kind == "tpT":
+                return [("tp", j), ("bias",)] + ([("ab", j - 2)] if j >= 2 else [])
+            if kind == "thT":
+                return [("th", j)] + ([("pr", j - 2)] if j >= 2 else [])
+            if kind == "ab":
+                return [("tpT", j)] + ([("sn", j - 3)] if j >= 3 else [])
+            if kind == "sn":
+                return [("ab", j)] + ([("pr", j - 3)] if j >= 3 else [])
+            if kind == "pr":
+                return [("sn",) + s[1:], ("thT", j)]
+            return []
+
+        def planes(c, ks):
+            return [("widen", c, k) for k in ks]
+
+        last = NT - 1
+        halves = ((0, HALF), (HALF, TOK))
+        scalar_q = planes(0, (4, 5, 6)) + [("xc", i) for i in range(NI)] + planes(1, (0, 1, 2, 3, 4)) + [("tp", 0)] + planes(1, (5,)) + [("tp", 1)]
+        scalar_fill = {1: planes(2, (0, 1, 2, 3)), 3: planes(3, (0, 1, 2, 3))}
+        for j in range(last):
+            scalar_q += [("ab", j)] + scalar_fill.get(j, []) + ([("tp", j + 1)] if j >= 1 else []) + [("th", j), ("sn", j)]
+        scalar_q += [("th", last), ("ab", last)] + [("sn", last) + h for h in halves]
+
+        vector_q = planes(0, (0, 1, 2, 3, 7)) + [("il", "p", 0), ("xq", 0, 0), ("xq", 0, 1), ("q", "p", 0), ("bias",), ("xq", 1, 0), ("xq", 1, 1), ("il", "a", 0)]
+        vector_q += planes(1, (6, 7)) + [("q", "a", 0)]
+        for c in range(1, NCH - 1):
+            vector_q += [("il", "p", c)] + planes(c + 1, (4, 5)) + [("q", "p", c)] + ([("pr", 2 * c - 3)] if c >= 2 else [])
+            vector_q += [("il", "a", c)] + planes(c + 1, (6, 7)) + [("q", "a", c), ("pr", 2 * c - 2)]
+        vector_q += [("il", "p", NCH - 1), ("pr", last - 4), ("q", "p", NCH - 1), ("il", "a", NCH - 1), ("pr", last - 3), ("q", "a", NCH - 1)]
+        vector_q += [("pr", last - 2), ("pr", last - 1)] + [("pr", last) + h for h in halves]
+
+        tensor_q = [("xT", i) for i in range(NI)] + [("bT",), ("mx", "p", 0), ("mx", "p", 1), ("tpT", 0), ("mx", "a", 0), ("tpT", 1), ("mx", "a", 1), ("thT", 0)]
+        for c in range(1, NCH):
+            a, b = 2 * c, 2 * c + 1
+            tensor_q += [("mx", "p", a), ("mx", "p", b), ("tpT", a), ("mx", "a", a), ("thT", a - 1), ("mx", "a", b), ("tpT", b), ("thT", a)]
+        tensor_q += [("thT", last)]
+
 
         nc.vector.memset(warm_in[:], 0.0)
         nc.vector.memset(brows[:], 0.0)
+        nc.vector.memset(ones_b[:], 1.0)
         nc.scalar.activation(out=warm_out[:], in_=warm_in[:], func=ACT.Silu)
         make_identity(nc, ident_b[:])
         make_identity(nc, ident_f[:])
 
         nc.sync.dma_start(out=ph_scale[:], in_=phs_v)
-        load_bytes(0)
-        load_bias()
-        for i in range(4):
+        load_bytes(0, 2)
+        for i in range(NI):
             load_x(i)
+        load_bias()
         load_amp(0)
-        load_bytes(1)
         load_amp(1)
+        load_bytes(2, 4)
         load_amp(2)
         load_amp(3)
 
-        widen(0, 0, False)
-        widen(0, 1, False)
-        widen(1, 0, True)
-        widen(1, 1, True, (0, 1))
-        interleave("p", 0)
-        bias_turn()
-        for i in range(3):
-            x_turn(i)
-            x_copy(i, True)
-        x_turn(3)
-        x_copy(3, True, 0, 1)
-        x_copy(3, True, 1, 2)
-        widen(1, 1, True, (2, 3))
-        widen(2, 0, True)
-        quantize("p", 0)
-        x_quantize(0)
-        x_quantize(1)
-        multiply("p", 0)
-        multiply("p", 1)
-        interleave("a", 0)
-        interleave("p", 1)
-        quantize("a", 0)
-        multiply("a", 0)
-        multiply("a", 1)
-
-        V_WIDEN = (2, 3)
-        S_OUT = (0, 1, 2, 3)
-        for c in range(NCH):
-            a, b = 2 * c, 2 * c + 1
-            last = c == NCH - 1
-            if not last and c > 0:
-                interleave("p", c + 1)
-            s_tp(a)
-            s_tp(b)
-            if c > 0:
-                product(b - 2)
-                turn_back(b - 2)
-            if not last:
-                quantize("p", c + 1)
-                multiply("p", a + 2)
-                multiply("p", b + 2)
-            s_ab(a)
-            s_ab(b)
-            s_sn(a)
-            if not last:
-                interleave("a", c + 1)
-            if c > 0:
-                copy_out(a - 2, a - 2 in S_OUT)
-            s_th(a)
-            if not last:
-                s_sn(b)
-            if c > 0:
-                copy_out(b - 2, b - 2 in S_OUT)
-            s_th(b)
-            product(a)
-            turn_back(a)
-            if not last:
-                quantize("a", c + 1)
-                multiply("a", a + 2)
-                multiply("a", b + 2)
-            if c + 2 in V_WIDEN:
-                if c + 2 > 2:
-                    widen(c + 2, 0, False)
-                widen(c + 2, 1, False)
-        j = NT - 1
-        s_sn(j, 0, 256)
-        s_sn(j, 256, 512)
-        product(j, 0, 256)
-        turn_back(j, 0, 256, True)
-        product(j, 256, 512)
-        turn_back(j, 256, 512, True)
-        copy_out(NT - 2, True)
-        copy_out(j, False, 0, 256)
-        copy_out(j, True, 256, 512)
+        queues = (scalar_q, vector_q, tensor_q)
+        heads = [0, 0, 0]
+        written = set()
+        while sum(heads) < sum(len(q) for q in queues):
+            before = sum(heads)
+            for e in range(3):
+                while heads[e] < len(queues[e]) and all(n in written for n in needs(queues[e][heads[e]])):
+                    s = queues[e][heads[e]]
+                    steps[s[0]](e == 0, *s[1:])
+                    written.add(s)
+                    heads[e] += 1
+            assert sum(heads) > before, "the queues wait for each other"

@@ -183,7 +183,11 @@ def tile_quantuminspiredneuralcore_pa_kernel(tc, x, amp_w, amp_b, ph_w_bytes, ph
                                            in1=ep[("thT", j)][:, lo:hi], op0=ALU.mult, op1=ALU.mult)
             nc.sync.dma_start(out=out_v[:, lo // P:hi // P, j * P:(j + 1) * P], in_=o_sb[:].rearrange("p (i n) -> p i n", n=P))
 
-        steps = {"bT": bias_turn, "bias": bias_copy, "widen": widen, "il": interleave, "q": quantize, "xT": x_turn, "xc": x_copy,
+        def warm_up(on_scalar, n):
+            dummy = psum.tile([P, TOK], F32, name="dummy_%d" % n, tag="thT")
+            nc.tensor.matmul(out=dummy[:], lhsT=ident_b[:], rhs=ones_b[:], start=True, stop=True)
+
+        steps = {"warm": warm_up, "bT": bias_turn, "bias": bias_copy, "widen": widen, "il": interleave, "q": quantize, "xT": x_turn, "xc": x_copy,
                  "xq": x_quantize, "mx": multiply, "tp": tanh_ph, "th": tanh_amp, "tpT": turn_ph, "thT": turn_amp, "ab": fold,
                  "sn": sine, "pr": product}
 
@@ -240,7 +244,7 @@ def tile_quantuminspiredneuralcore_pa_kernel(tc, x, amp_w, amp_b, ph_w_bytes, ph
         vector_q += [("il", "p", NCH - 1), ("pr", last - 4), ("q", "p", NCH - 1), ("il", "a", NCH - 1), ("pr", last - 3), ("q", "a", NCH - 1)]
         vector_q += [("pr", last - 2), ("pr", last - 1)] + [("pr", last) + h for h in halves]
 
-        tensor_q = [("xT", i) for i in range(NI)] + [("bT",), ("mx", "p", 0), ("mx", "p", 1), ("tpT", 0), ("mx", "a", 0), ("tpT", 1), ("mx", "a", 1), ("thT", 0)]
+        tensor_q = [("warm", 0), ("warm", 1)] + [("xT", i) for i in range(NI)] + [("bT",), ("warm", 2), ("warm", 3), ("mx", "p", 0), ("mx", "p", 1), ("tpT", 0), ("mx", "a", 0), ("tpT", 1), ("mx", "a", 1), ("thT", 0)]
         for c in range(1, NCH):
             a, b = 2 * c, 2 * c + 1
             tensor_q += [("mx", "p", a), ("mx", "p", b), ("tpT", a), ("mx", "a", a), ("thT", a - 1), ("mx", "a", b), ("tpT", b), ("thT", a)]

@@ -67,10 +67,12 @@ def tile_quantuminspiredneuralcore_pa_kernel(tc, x, amp_w, amp_b, ph_w_bytes, ph
         acc = {}
         ep = {}
 
-        def load_bytes(c0, c1):
+        def load_bytes(c0, c1, pieces=1):
             for g in range(G):
                 both = keep.tile([P, T, (c1 - c0) * NW], U8, name="ph_bytes_%d_%d" % (c0, g))
-                nc.sync.dma_start(out=both[:], in_=phb_v[g][:, :, c0 * NW:c1 * NW])
+                step = T // pieces
+                for t0 in range(0, T, step):
+                    nc.sync.dma_start(out=both[:, t0:t0 + step, :], in_=phb_v[g][:, t0:t0 + step, c0 * NW:c1 * NW])
                 for c in range(c0, c1):
                     ph_bytes[(c, g)] = both[:, :, (c - c0) * NW:(c - c0 + 1) * NW]
 
@@ -185,14 +187,29 @@ def tile_quantuminspiredneuralcore_pa_kernel(tc, x, amp_w, amp_b, ph_w_bytes, ph
 
         def warm_up(on_scalar, n):
             dummy = psum.tile([P, TOK], F32, name="dummy_%d" % n, tag="thT")
-            nc.tensor.matmul(out=dummy[:], lhsT=ident_b[:], rhs=ones_b[:], start=True, stop=True)
+            nc.tensor.matmul(out=dummy[:, 0:P], lhsT=ident_f[:], rhs=ident_f[:], start=True, stop=True)
 
-        steps = {"warm": warm_up, "bT": bias_turn, "bias": bias_copy, "widen": widen, "il": interleave, "q": quantize, "xT": x_turn, "xc": x_copy,
+        def half_sine(on_scalar, j):
+            nc.scalar.activation(out=new("ab", j)[:], in_=ep[("tpT", j)][:], func=ACT.Sin, bias=-math.pi / 8, scale=math.pi / 2)
+
+        def square(on_scalar, j, lo=0, hi=TOK):
+            if lo == 0:
+                new("sn", j)
+            nc.vector.scalar_tensor_tensor(out=ep[("sn", j)][:, lo:hi], in0=ep[("ab", j)][:, lo:hi], scalar=-math.sqrt(2.0),
+                                           in1=ep[("ab", j)][:, lo:hi], op0=ALU.mult, op1=ALU.mult)
+
+        def product_cos(on_scalar, j, lo=0, hi=TOK):
+            o_sb = work.tile([P, hi - lo], F32, name="o_sb_%d_%d" % (j, lo), tag="o_sb", bufs=4)
+            nc.vector.scalar_tensor_tensor(out=o_sb[:], in0=ep[("sn", j)][:, lo:hi], scalar=math.sqrt(0.5),
+                                           in1=ep[("thT", j)][:, lo:hi], op0=ALU.add, op1=ALU.mult)
+            nc.sync.dma_start(out=out_v[:, lo // P:hi // P, j * P:(j + 1) * P], in_=o_sb[:].rearrange("p (i n) -> p i n", n=P))
+
+        steps = {"hs": half_sine, "sq": square, "pc": product_cos, "warm": warm_up, "bT": bias_turn, "bias": bias_copy, "widen": widen, "il": interleave, "q": quantize, "xT": x_turn, "xc": x_copy,
                  "xq": x_quantize, "mx": multiply, "tp": tanh_ph, "th": tanh_amp, "tpT": turn_ph, "thT": turn_amp, "ab": fold,
                  "sn": sine, "pr": product}
 
         def needs(s):
-            kind = s[0]
+            kind = {"hs": "ab", "sq": "sn", "pc": "pr"}.get(s[0], s[0])
             j = s[2] if kind in ("il", "q", "mx") else s[-1] if len(s) == 2 else s[1] if len(s) > 1 else 0
             x_done = [("xq", h, g) for h in range(2) for g in range(G)]
             if kind == "il":
@@ -230,21 +247,30 @@ def tile_quantuminspiredneuralcore_pa_kernel(tc, x, amp_w, amp_b, ph_w_bytes, ph
 
         last = NT - 1
         halves = ((0, HALF), (HALF, TOK))
-        scalar_q = planes(0, (4, 5, 6)) + [("xc", i) for i in range(NI)] + planes(1, (0, 1, 2, 3, 4)) + [("tp", 0)] + planes(1, (5,)) + [("tp", 1)]
+        by_square = ()
+        scalar_q = planes(0, (4, 5, 6)) + planes(1, ()) + [("xc", i) for i in range(NI)] + planes(1, (0, 1, 2, 3, 4)) + [("tp", 0)] + planes(1, (5,)) + [("tp", 1)]
         scalar_fill = {1: planes(2, (0, 1, 2, 3)), 3: planes(3, (0, 1, 2, 3))}
         for j in range(last):
-            scalar_q += [("ab", j)] + scalar_fill.get(j, []) + ([("tp", j + 1)] if j >= 1 else []) + [("th", j), ("sn", j)]
-        scalar_q += [("th", last), ("ab", last)] + [("sn", last) + h for h in halves]
+            scalar_q += [("hs" if j in by_square else "ab", j)] + scalar_fill.get(j, []) + ([("tp", j + 1)] if j >= 1 else []) + [("th", j)]
+            scalar_q += [] if j in by_square else [("sn", j)]
+        scalar_q += [("th", last)] + ([("hs", last)] if last in by_square else [("ab", last)] + [("sn", last) + h for h in halves])
 
-        vector_q = planes(0, (0, 1, 2, 3, 7)) + [("il", "p", 0), ("xq", 0, 0), ("xq", 0, 1), ("q", "p", 0), ("bias",), ("xq", 1, 0), ("xq", 1, 1), ("il", "a", 0)]
-        vector_q += planes(1, (6, 7)) + [("q", "a", 0)]
+        def finish(j):
+            return [("sq", j), ("pc", j)] if j in by_square else [("pr", j)]
+
+        vector_q = planes(0, (0, 1, 2, 3, 7)) + [("il", "p", 0), ("xq", 0, 0), ("xq", 0, 1), ("q", "p", 0), ("bias",), ("xq", 1, 0), ("xq", 1, 1), ("il", "a", 0)] + planes(1, (6, 7)) + [("q", "a", 0)]
+        vector_planes = {2: (4, 5, 6, 7), 3: (4, 5, 6, 7)}
         for c in range(1, NCH - 1):
-            vector_q += [("il", "p", c)] + planes(c + 1, (4, 5)) + [("q", "p", c)] + ([("pr", 2 * c - 3)] if c >= 2 else [])
-            vector_q += [("il", "a", c)] + planes(c + 1, (6, 7)) + [("q", "a", c), ("pr", 2 * c - 2)]
-        vector_q += [("il", "p", NCH - 1), ("pr", last - 4), ("q", "p", NCH - 1), ("il", "a", NCH - 1), ("pr", last - 3), ("q", "a", NCH - 1)]
-        vector_q += [("pr", last - 2), ("pr", last - 1)] + [("pr", last) + h for h in halves]
+            mine = vector_planes[c + 1]
+            vector_q += [("il", "p", c)] + planes(c + 1, mine[:len(mine) // 2]) + [("q", "p", c)] + (finish(2 * c - 3) if c >= 2 else [])
+            vector_q += [("il", "a", c)] + planes(c + 1, mine[len(mine) // 2:]) + [("q", "a", c)] + finish(2 * c - 2)
+        vector_q += [("il", "p", NCH - 1)] + finish(last - 4) + [("q", "p", NCH - 1), ("il", "a", NCH - 1)] + finish(last - 3) + [("q", "a", NCH - 1)]
+        vector_q += finish(last - 2) + finish(last - 1)
+        for h in halves:
+            vector_q += [("sq", last) + h, ("pc", last) + h] if last in by_square else [("pr", last) + h]
 
-        tensor_q = [("warm", 0), ("warm", 1)] + [("xT", i) for i in range(NI)] + [("bT",), ("warm", 2), ("warm", 3), ("mx", "p", 0), ("mx", "p", 1), ("tpT", 0), ("mx", "a", 0), ("tpT", 1), ("mx", "a", 1), ("thT", 0)]
+        tensor_q = [("warm", n) for n in range(3)] + [("xT", 0), ("warm", 3), ("xT", 1), ("warm", 4), ("xT", 2), ("xT", 3), ("bT",)] + [("warm", n) for n in range(5, 8)]
+        tensor_q += [("mx", "p", 0), ("mx", "p", 1), ("tpT", 0), ("mx", "a", 0), ("tpT", 1), ("mx", "a", 1), ("thT", 0)]
         for c in range(1, NCH):
             a, b = 2 * c, 2 * c + 1
             tensor_q += [("mx", "p", a), ("mx", "p", b), ("tpT", a), ("mx", "a", a), ("thT", a - 1), ("mx", "a", b), ("tpT", b), ("thT", a)]
@@ -255,8 +281,8 @@ def tile_quantuminspiredneuralcore_pa_kernel(tc, x, amp_w, amp_b, ph_w_bytes, ph
         nc.vector.memset(brows[:], 0.0)
         nc.vector.memset(ones_b[:], 1.0)
         nc.scalar.activation(out=warm_out[:], in_=warm_in[:], func=ACT.Silu)
-        make_identity(nc, ident_b[:])
         make_identity(nc, ident_f[:])
+        make_identity(nc, ident_b[:])
 
         nc.sync.dma_start(out=ph_scale[:], in_=phs_v)
         load_bytes(0, 2)
@@ -269,6 +295,7 @@ def tile_quantuminspiredneuralcore_pa_kernel(tc, x, amp_w, amp_b, ph_w_bytes, ph
         load_amp(2)
         load_amp(3)
 
+        alias = {"hs": "ab", "sq": "sn", "pc": "pr"}
         queues = (scalar_q, vector_q, tensor_q)
         heads = [0, 0, 0]
         written = set()
@@ -278,6 +305,6 @@ def tile_quantuminspiredneuralcore_pa_kernel(tc, x, amp_w, amp_b, ph_w_bytes, ph
                 while heads[e] < len(queues[e]) and all(n in written for n in needs(queues[e][heads[e]])):
                     s = queues[e][heads[e]]
                     steps[s[0]](e == 0, *s[1:])
-                    written.add(s)
+                    written.add((alias.get(s[0], s[0]),) + s[1:])
                     heads[e] += 1
             assert sum(heads) > before, "the queues wait for each other"

@@ -52,10 +52,9 @@ def tile_quantuminspiredneuralcore_pa_kernel(tc, x, amp_w, amp_b, ph_w_bytes, ph
         ones_b = keep.tile([P, TOK], BF16, name="ones_b")
         ph_scale = keep.tile([P, G, T], F32, name="ph_scale")
         bias = keep.tile([P, 2 * NT], F32, name="bias")
-        x_grouped = keep.tile([P, G, TOK, T], BF16, name="x_grouped", align_bytes=64)
+        x_grouped = [keep.tile([P, G, HALF, T], BF16, name="x_grouped_%d" % h, align_bytes=64) for h in range(2)]
         x_codes = keep.tile([P, G, TOK], U32, name="x_codes", align_bytes=64)
         x_scales = keep.tile([P, G, TOK], U8, name="x_scales", align_bytes=64)
-        xg_words = x_grouped[:].bitcast(F32)
 
         ph_bytes = {}
         raw = {}
@@ -127,7 +126,8 @@ def tile_quantuminspiredneuralcore_pa_kernel(tc, x, amp_w, amp_b, ph_w_bytes, ph
                     nc.tensor.transpose(xt[i][:, g, u, :], words[:, 256 * g + u:256 * (g + 1):2], ident_f[:])
 
         def x_copy(on_scalar, i):
-            dst = xg_words[:, :, i * P:(i + 1) * P, :]
+            h, q = divmod(i, 2)
+            dst = x_grouped[h][:].bitcast(F32)[:, :, q * P:(q + 1) * P, :]
             src = xt[i][:].rearrange("p g u r -> p g r u")
             if on_scalar:
                 nc.scalar.copy(out=dst, in_=src)
@@ -137,7 +137,7 @@ def tile_quantuminspiredneuralcore_pa_kernel(tc, x, amp_w, amp_b, ph_w_bytes, ph
         def x_quantize(on_scalar, h, g):
             lo, hi = h * HALF, (h + 1) * HALF
             nc.vector.quantize_mx(out=x_codes[:, g, lo:hi].bitcast(FP8X4), scales=x_scales[:, g, lo:hi],
-                                  in_=x_grouped[:, g, lo:hi].rearrange("p r t -> p (r t)"))
+                                  in_=x_grouped[h][:, g].rearrange("p r t -> p (r t)"))
 
         def multiply(on_scalar, w, j):
             c, h = divmod(j, TPC)

@@ -40,7 +40,7 @@ def tile_quantuminspiredneuralcore_pa_kernel(tc, x, amp_w, amp_b, ph_w_bytes, ph
 
     with ExitStack() as ctx:
         keep = ctx.enter_context(tc.tile_pool(name="keep", bufs=1))
-        work = ctx.enter_context(tc.tile_pool(name="work", bufs=3))
+        work = ctx.enter_context(tc.tile_pool(name="work", bufs=5))
         psum = ctx.enter_context(tc.psum_pool(name="psum", bufs=2))
         ctx.enter_context(tc.manual_schedule())
 
@@ -56,6 +56,7 @@ def tile_quantuminspiredneuralcore_pa_kernel(tc, x, amp_w, amp_b, ph_w_bytes, ph
         x_codes = keep.tile([P, G, TOK], U32, name="x_codes", align_bytes=64)
         x_scales = keep.tile([P, G, TOK], U8, name="x_scales", align_bytes=64)
 
+        paired = (1, 2)
         ph_bytes = {}
         raw = {}
         x_sb = {}
@@ -98,10 +99,11 @@ def tile_quantuminspiredneuralcore_pa_kernel(tc, x, amp_w, amp_b, ph_w_bytes, ph
 
         def widen(on_scalar, c, k):
             if ("p", c) not in raw:
-                raw[("p", c)] = keep.tile([P, T, G, NW], BF16, name="ph_wide_%d" % c)
+                shape = [P, 2, G, NW, 2] if c in paired else [P, T, G, NW]
+                raw[("p", c)] = keep.tile(shape, BF16, name="ph_wide_%d" % c)
             g, t = divmod(k, T)
             src = ph_bytes[(c, g)][:, t, :].bitcast(FP8)
-            dst = raw[("p", c)][:, t, g, :]
+            dst = raw[("p", c)][:, t // 2, g, :, t % 2] if c in paired else raw[("p", c)][:, t, g, :]
             if on_scalar:
                 nc.scalar.activation(out=dst, in_=src, func=ACT.Copy, scale=ph_scale[:, g, t:t + 1])
             else:
@@ -109,8 +111,12 @@ def tile_quantuminspiredneuralcore_pa_kernel(tc, x, amp_w, amp_b, ph_w_bytes, ph
 
         def interleave(on_scalar, w, c):
             grouped[(w, c)] = keep.tile([P, G * NW, T], BF16, name="grouped_%s_%d" % (w, c), align_bytes=64)
-            nc.vector.tensor_copy(out=grouped[(w, c)][:].rearrange("p (c i) t -> p c t i", i=4),
-                                  in_=raw[(w, c)][:].rearrange("p t g n -> p t (g n)").rearrange("p t (c i) -> p c t i", i=4))
+            if w == "p" and c in paired:
+                nc.vector.tensor_copy(out=grouped[(w, c)][:].rearrange("p m (u e) -> p m u e", e=2),
+                                      in_=raw[(w, c)][:].rearrange("p u g n e -> p u (g n) e").rearrange("p u m e -> p m u e"))
+            else:
+                nc.vector.tensor_copy(out=grouped[(w, c)][:].rearrange("p (c i) t -> p c t i", i=4),
+                                      in_=raw[(w, c)][:].rearrange("p t g n -> p t (g n)").rearrange("p t (c i) -> p c t i", i=4))
 
         def quantize(on_scalar, w, c):
             codes[(w, c)] = keep.tile([P, G * NW], U32, name="codes_%s_%d" % (w, c), align_bytes=64)
@@ -189,35 +195,18 @@ def tile_quantuminspiredneuralcore_pa_kernel(tc, x, amp_w, amp_b, ph_w_bytes, ph
             dummy = psum.tile([P, TOK], F32, name="dummy_%d" % n, tag="thT")
             nc.tensor.matmul(out=dummy[:, 0:P], lhsT=ident_f[:], rhs=ident_f[:], start=True, stop=True)
 
-        def half_sine(on_scalar, j):
-            nc.scalar.activation(out=new("ab", j)[:], in_=ep[("tpT", j)][:], func=ACT.Sin, bias=-math.pi / 8, scale=math.pi / 2)
-
-        def square(on_scalar, j, lo=0, hi=TOK):
-            if lo == 0:
-                new("sn", j)
-            nc.vector.scalar_tensor_tensor(out=ep[("sn", j)][:, lo:hi], in0=ep[("ab", j)][:, lo:hi], scalar=-math.sqrt(2.0),
-                                           in1=ep[("ab", j)][:, lo:hi], op0=ALU.mult, op1=ALU.mult)
-
-        def product_cos(on_scalar, j, lo=0, hi=TOK):
-            o_sb = work.tile([P, hi - lo], F32, name="o_sb_%d_%d" % (j, lo), tag="o_sb", bufs=4)
-            nc.vector.scalar_tensor_tensor(out=o_sb[:], in0=ep[("sn", j)][:, lo:hi], scalar=math.sqrt(0.5),
-                                           in1=ep[("thT", j)][:, lo:hi], op0=ALU.add, op1=ALU.mult)
-            nc.sync.dma_start(out=out_v[:, lo // P:hi // P, j * P:(j + 1) * P], in_=o_sb[:].rearrange("p (i n) -> p i n", n=P))
-
-        steps = {"hs": half_sine, "sq": square, "pc": product_cos, "warm": warm_up, "bT": bias_turn, "bias": bias_copy, "widen": widen, "il": interleave, "q": quantize, "xT": x_turn, "xc": x_copy,
+        steps = {"warm": warm_up, "bT": bias_turn, "bias": bias_copy, "widen": widen, "il": interleave, "q": quantize, "xT": x_turn, "xc": x_copy,
                  "xq": x_quantize, "mx": multiply, "tp": tanh_ph, "th": tanh_amp, "tpT": turn_ph, "thT": turn_amp, "ab": fold,
                  "sn": sine, "pr": product}
 
         def needs(s):
-            kind = {"hs": "ab", "sq": "sn", "pc": "pr"}.get(s[0], s[0])
+            kind = s[0]
             j = s[2] if kind in ("il", "q", "mx") else s[-1] if len(s) == 2 else s[1] if len(s) > 1 else 0
             x_done = [("xq", h, g) for h in range(2) for g in range(G)]
             if kind == "il":
                 return [("widen", j, k) for k in range(G * T)] if s[1] == "p" else []
             if kind == "q":
                 return [("il", s[1], j)]
-            if kind == "xT":
-                return [("xc", j - 2)] if j >= 2 else []
             if kind == "xc":
                 return [("xT", j)]
             if kind == "xq":
@@ -246,36 +235,35 @@ def tile_quantuminspiredneuralcore_pa_kernel(tc, x, amp_w, amp_b, ph_w_bytes, ph
             return [("widen", c, k) for k in ks]
 
         last = NT - 1
-        halves = ((0, HALF), (HALF, TOK))
-        by_square = ()
-        scalar_q = planes(0, (4, 5, 6)) + planes(1, ()) + [("xc", i) for i in range(NI)] + planes(1, (0, 1, 2, 3, 4)) + [("tp", 0)] + planes(1, (5,)) + [("tp", 1)]
-        scalar_fill = {1: planes(2, (0, 1, 2, 3)), 3: planes(3, (0, 1, 2, 3))}
-        for j in range(last):
-            scalar_q += [("hs" if j in by_square else "ab", j)] + scalar_fill.get(j, []) + ([("tp", j + 1)] if j >= 1 else []) + [("th", j)]
-            scalar_q += [] if j in by_square else [("sn", j)]
-        scalar_q += [("th", last)] + ([("hs", last)] if last in by_square else [("ab", last)] + [("sn", last) + h for h in halves])
+        by_scalar = {0: (2, 3, 4, 5, 6, 7), 1: (), 2: (), 3: (2, 3, 4, 5, 6, 7)}
+        by_vector = {c: tuple(k for k in (0, 2, 1, 3, 4, 6, 5, 7) if k not in by_scalar[c]) for c in range(NCH)}
 
         def finish(j):
-            return [("sq", j), ("pc", j)] if j in by_square else [("pr", j)]
+            return [("pr", j)] if j < last else [("pr", j, 0, HALF), ("pr", j, HALF, TOK)]
 
-        vector_q = planes(0, (0, 1, 2, 3, 7)) + [("il", "p", 0), ("xq", 0, 0), ("xq", 0, 1), ("q", "p", 0), ("bias",), ("xq", 1, 0), ("xq", 1, 1), ("il", "a", 0)] + planes(1, (6, 7)) + [("q", "a", 0)]
-        vector_planes = {2: (4, 5, 6, 7), 3: (4, 5, 6, 7)}
-        for c in range(1, NCH - 1):
-            mine = vector_planes[c + 1]
-            vector_q += [("il", "p", c)] + planes(c + 1, mine[:len(mine) // 2]) + [("q", "p", c)] + (finish(2 * c - 3) if c >= 2 else [])
-            vector_q += [("il", "a", c)] + planes(c + 1, mine[len(mine) // 2:]) + [("q", "a", c)] + finish(2 * c - 2)
-        vector_q += [("il", "p", NCH - 1)] + finish(last - 4) + [("q", "p", NCH - 1), ("il", "a", NCH - 1)] + finish(last - 3) + [("q", "a", NCH - 1)]
-        vector_q += finish(last - 2) + finish(last - 1)
-        for h in halves:
-            vector_q += [("sq", last) + h, ("pc", last) + h] if last in by_square else [("pr", last) + h]
-
+        scalar_q = planes(0, by_scalar[0]) + [("xc", i) for i in range(NI)] + planes(3, by_scalar[3])
+        vector_q = planes(0, by_vector[0]) + planes(1, by_vector[1][:-1]) + [("il", "p", 0)] + planes(1, by_vector[1][-1:]) + [("q", "p", 0)]
+        vector_q += [("xq", h, g) for h in range(2) for g in range(G)] + [("bias",)]
         tensor_q = [("warm", n) for n in range(3)] + [("xT", 0), ("warm", 3), ("xT", 1), ("warm", 4), ("xT", 2), ("xT", 3), ("bT",)] + [("warm", n) for n in range(5, 8)]
-        tensor_q += [("mx", "p", 0), ("mx", "p", 1), ("tpT", 0), ("mx", "a", 0), ("tpT", 1), ("mx", "a", 1), ("thT", 0)]
-        for c in range(1, NCH):
-            a, b = 2 * c, 2 * c + 1
-            tensor_q += [("mx", "p", a), ("mx", "p", b), ("tpT", a), ("mx", "a", a), ("thT", a - 1), ("mx", "a", b), ("tpT", b), ("thT", a)]
-        tensor_q += [("thT", last)]
-
+        for c in range(NCH):
+            new_tiles = [2 * c, 2 * c + 1]
+            old_tiles = [2 * c - 2, 2 * c - 1] if c else []
+            tensor_q += [("mx", "p", j) for j in new_tiles] + [("mx", "a", j) for j in old_tiles]
+            tensor_q += [("tpT", j) for j in new_tiles] + [("thT", j) for j in old_tiles]
+            scalar_q += [("tp", j) for j in new_tiles] + [("th", j) for j in old_tiles]
+            scalar_q += [("ab", j) for j in new_tiles]
+            for j in new_tiles:
+                scalar_q += [("sn", j)] if j < last else [("th", last - 1), ("th", last), ("sn", j, 0, HALF), ("sn", j, HALF, TOK)]
+            if c + 1 < NCH:
+                vector_q += [("il", "p", c + 1), ("il", "a", c), ("q", "p", c + 1), ("q", "a", c)]
+            else:
+                vector_q += [("il", "a", c), ("q", "a", c)]
+            for j in old_tiles:
+                vector_q += finish(j)
+            if c + 2 < NCH:
+                vector_q += planes(c + 2, by_vector[c + 2])
+        vector_q += finish(last - 1) + finish(last)
+        tensor_q += [("mx", "a", last - 1), ("mx", "a", last), ("thT", last - 1), ("thT", last)]
 
         nc.vector.memset(warm_in[:], 0.0)
         nc.vector.memset(brows[:], 0.0)
@@ -290,12 +278,10 @@ def tile_quantuminspiredneuralcore_pa_kernel(tc, x, amp_w, amp_b, ph_w_bytes, ph
             load_x(i)
         load_bias()
         load_amp(0)
-        load_amp(1)
         load_bytes(2, 4)
-        load_amp(2)
-        load_amp(3)
+        for c in range(1, NCH):
+            load_amp(c)
 
-        alias = {"hs": "ab", "sq": "sn", "pc": "pr"}
         queues = (scalar_q, vector_q, tensor_q)
         heads = [0, 0, 0]
         written = set()
@@ -305,6 +291,6 @@ def tile_quantuminspiredneuralcore_pa_kernel(tc, x, amp_w, amp_b, ph_w_bytes, ph
                 while heads[e] < len(queues[e]) and all(n in written for n in needs(queues[e][heads[e]])):
                     s = queues[e][heads[e]]
                     steps[s[0]](e == 0, *s[1:])
-                    written.add((alias.get(s[0], s[0]),) + s[1:])
+                    written.add(s)
                     heads[e] += 1
             assert sum(heads) > before, "the queues wait for each other"

@@ -27,6 +27,7 @@ NT = N // P
 TPC = NW // P
 NI = TOK // P
 HALF = TOK // 2
+DEPTH = 5
 
 
 def tile_quantuminspiredneuralcore_pa_kernel(tc, x, amp_w, amp_b, ph_w_bytes, ph_w_scale, ph_b, out):
@@ -40,7 +41,7 @@ def tile_quantuminspiredneuralcore_pa_kernel(tc, x, amp_w, amp_b, ph_w_bytes, ph
 
     with ExitStack() as ctx:
         keep = ctx.enter_context(tc.tile_pool(name="keep", bufs=1))
-        work = ctx.enter_context(tc.tile_pool(name="work", bufs=5))
+        work = ctx.enter_context(tc.tile_pool(name="work", bufs=DEPTH))
         psum = ctx.enter_context(tc.psum_pool(name="psum", bufs=2))
         ctx.enter_context(tc.manual_schedule())
 
@@ -56,7 +57,8 @@ def tile_quantuminspiredneuralcore_pa_kernel(tc, x, amp_w, amp_b, ph_w_bytes, ph
         x_codes = keep.tile([P, G, TOK], U32, name="x_codes", align_bytes=64)
         x_scales = keep.tile([P, G, TOK], U8, name="x_scales", align_bytes=64)
 
-        paired = (1, 2)
+        by_half = (5,)
+        paired = (1, 3)
         ph_bytes = {}
         raw = {}
         x_sb = {}
@@ -171,7 +173,7 @@ def tile_quantuminspiredneuralcore_pa_kernel(tc, x, amp_w, amp_b, ph_w_bytes, ph
                 nc.tensor.transpose(ep[("tpT", j)][:, i * P:(i + 1) * P], ep[("tp", j)][:, i * P:(i + 1) * P], ident_f[:])
 
         def turn_amp(on_scalar, j):
-            ep[("thT", j)] = psum.tile([P, TOK], F32, name="thT_%d" % j, tag="thT")
+            ep[("thT", j)] = psum.tile([P, TOK], F32, name="thT_%d" % j, tag="thT" if j < NT - TPC else "tpT")
             nc.tensor.matmul(out=ep[("thT", j)][:], lhsT=ident_b[:], rhs=ones_b[:], start=True, stop=False)
             for i in range(NI):
                 nc.tensor.matmul(out=ep[("thT", j)][:, i * P:(i + 1) * P], lhsT=ep[("th", j)][:, i * P:(i + 1) * P], rhs=ident_f[:],
@@ -180,6 +182,13 @@ def tile_quantuminspiredneuralcore_pa_kernel(tc, x, amp_w, amp_b, ph_w_bytes, ph
         def fold(on_scalar, j):
             nc.scalar.activation(out=new("ab", j)[:], in_=ep[("tpT", j)][:], func=ACT.Abs, bias=-0.25, scale=1.0)
 
+        def half_sine(on_scalar, j):
+            nc.scalar.activation(out=new("sn", j)[:], in_=ep[("tpT", j)][:], func=ACT.Sin, bias=-math.pi / 8, scale=math.pi / 2)
+
+        def square(on_scalar, j):
+            nc.vector.scalar_tensor_tensor(out=new("sq", j)[:], in0=ep[("sn", j)][:], scalar=-math.sqrt(2.0), in1=ep[("sn", j)][:],
+                                           op0=ALU.mult, op1=ALU.mult)
+
         def sine(on_scalar, j, lo=0, hi=TOK):
             if lo == 0:
                 new("sn", j)
@@ -187,8 +196,9 @@ def tile_quantuminspiredneuralcore_pa_kernel(tc, x, amp_w, amp_b, ph_w_bytes, ph
 
         def product(on_scalar, j, lo=0, hi=TOK):
             o_sb = work.tile([P, hi - lo], F32, name="o_sb_%d_%d" % (j, lo), tag="o_sb", bufs=4)
-            nc.vector.scalar_tensor_tensor(out=o_sb[:], in0=ep[("sn", j)][:, lo:hi], scalar=math.sqrt(0.5),
-                                           in1=ep[("thT", j)][:, lo:hi], op0=ALU.mult, op1=ALU.mult)
+            kind, first = ("sq", ALU.add) if j in by_half else ("sn", ALU.mult)
+            nc.vector.scalar_tensor_tensor(out=o_sb[:], in0=ep[(kind, j)][:, lo:hi], scalar=math.sqrt(0.5),
+                                           in1=ep[("thT", j)][:, lo:hi], op0=first, op1=ALU.mult)
             nc.sync.dma_start(out=out_v[:, lo // P:hi // P, j * P:(j + 1) * P], in_=o_sb[:].rearrange("p (i n) -> p i n", n=P))
 
         def warm_up(on_scalar, n):
@@ -197,7 +207,7 @@ def tile_quantuminspiredneuralcore_pa_kernel(tc, x, amp_w, amp_b, ph_w_bytes, ph
 
         steps = {"warm": warm_up, "bT": bias_turn, "bias": bias_copy, "widen": widen, "il": interleave, "q": quantize, "xT": x_turn, "xc": x_copy,
                  "xq": x_quantize, "mx": multiply, "tp": tanh_ph, "th": tanh_amp, "tpT": turn_ph, "thT": turn_amp, "ab": fold,
-                 "sn": sine, "pr": product}
+                 "hs": half_sine, "sq": square, "sn": sine, "pr": product}
 
         def needs(s):
             kind = s[0]
@@ -216,54 +226,63 @@ def tile_quantuminspiredneuralcore_pa_kernel(tc, x, amp_w, amp_b, ph_w_bytes, ph
             if kind == "mx":
                 return [("q", s[1], j // TPC)] + x_done + ([({"p": "tp", "a": "th"}[s[1]], j - 2)] if j >= 2 else [])
             if kind == "tp":
-                return [("mx", "p", j), ("bias",)] + ([("tpT", j - 3)] if j >= 3 else [])
+                return [("mx", "p", j), ("bias",)] + ([("tpT", j - DEPTH)] if j >= DEPTH else [])
             if kind == "th":
-                return [("mx", "a", j), ("bias",)] + ([("thT", j - 3)] if j >= 3 else [])
+                return [("mx", "a", j), ("bias",)] + ([("thT", j - DEPTH)] if j >= DEPTH else [])
             if kind == "tpT":
-                return [("tp", j), ("bias",)] + ([("ab", j - 2)] if j >= 2 else [])
+                return [("tp", j), ("bias",)] + ([fold_of(j - 2)] if j >= 2 else [])
             if kind == "thT":
-                return [("th", j)] + ([("pr", j - 2)] if j >= 2 else [])
+                return [("th", j)] + ([fold_of(j)] if j >= NT - TPC else [("pr", j - 2)] if j >= 2 else [])
             if kind == "ab":
-                return [("tpT", j)] + ([("sn", j - 3)] if j >= 3 else [])
+                return [("tpT", j)] + ([("sn", j - DEPTH)] if j >= DEPTH and j - DEPTH not in by_half else [])
             if kind == "sn":
-                return [("ab", j)] + ([("pr", j - 3)] if j >= 3 else [])
+                return [("ab", j)] + ([("pr", j - DEPTH + 1)] if j >= DEPTH - 1 else [])
+            if kind == "hs":
+                return [("tpT", j)] + ([("pr", j - DEPTH + 1)] if j >= DEPTH - 1 else [])
+            if kind == "sq":
+                return [("hs", j)]
             if kind == "pr":
-                return [("sn",) + s[1:], ("thT", j)]
+                return [("sq", j) if j in by_half else ("sn",) + s[1:], ("thT", j)]
             return []
+
+        def fold_of(j):
+            return ("hs", j) if j in by_half else ("ab", j)
 
         def planes(c, ks):
             return [("widen", c, k) for k in ks]
 
         last = NT - 1
-        by_scalar = {0: (2, 3, 4, 5, 6, 7), 1: (), 2: (), 3: (2, 3, 4, 5, 6, 7)}
+        by_scalar = {0: (2, 3, 4, 5, 6, 7), 1: (), 2: (2, 3, 4, 5, 6, 7), 3: ()}
         by_vector = {c: tuple(k for k in (0, 2, 1, 3, 4, 6, 5, 7) if k not in by_scalar[c]) for c in range(NCH)}
 
         def finish(j):
-            return [("pr", j)] if j < last else [("pr", j, 0, HALF), ("pr", j, HALF, TOK)]
+            return [("sq", j), ("pr", j)] if j in by_half else [("pr", j)] if j < last else [("pr", j, 0, HALF), ("pr", j, HALF, TOK)]
 
-        scalar_q = planes(0, by_scalar[0]) + [("xc", i) for i in range(NI)] + planes(3, by_scalar[3])
+        scalar_q = planes(0, by_scalar[0]) + [("xc", i) for i in range(NI)] + planes(2, by_scalar[2])
         vector_q = planes(0, by_vector[0]) + planes(1, by_vector[1][:-1]) + [("il", "p", 0)] + planes(1, by_vector[1][-1:]) + [("q", "p", 0)]
         vector_q += [("xq", h, g) for h in range(2) for g in range(G)] + [("bias",)]
         tensor_q = [("warm", n) for n in range(3)] + [("xT", 0), ("warm", 3), ("xT", 1), ("warm", 4), ("xT", 2), ("xT", 3), ("bT",)] + [("warm", n) for n in range(5, 8)]
+        products = [s for j in range(NT) for s in finish(j)]
         for c in range(NCH):
             new_tiles = [2 * c, 2 * c + 1]
             old_tiles = [2 * c - 2, 2 * c - 1] if c else []
-            tensor_q += [("mx", "p", j) for j in new_tiles] + [("mx", "a", j) for j in old_tiles]
-            tensor_q += [("tpT", j) for j in new_tiles] + [("thT", j) for j in old_tiles]
+            tensor_q += [("mx", "p", j) for j in new_tiles]
+            tensor_q += [("thT", j - 2) for j in old_tiles if j >= 2]
+            tensor_q += [("mx", "a", j) for j in old_tiles] + [("tpT", j) for j in new_tiles]
             scalar_q += [("tp", j) for j in new_tiles] + [("th", j) for j in old_tiles]
-            scalar_q += [("ab", j) for j in new_tiles]
+            scalar_q += [fold_of(j) for j in new_tiles]
             for j in new_tiles:
-                scalar_q += [("sn", j)] if j < last else [("th", last - 1), ("th", last), ("sn", j, 0, HALF), ("sn", j, HALF, TOK)]
-            if c + 1 < NCH:
-                vector_q += [("il", "p", c + 1), ("il", "a", c), ("q", "p", c + 1), ("q", "a", c)]
-            else:
-                vector_q += [("il", "a", c), ("q", "a", c)]
-            for j in old_tiles:
-                vector_q += finish(j)
+                scalar_q += [] if j in by_half else [("sn", j)] if j < last else [("th", last - 1), ("th", last), ("sn", j, 0, HALF), ("sn", j, HALF, TOK)]
+            weights = ([("p", c + 1)] if c + 1 < NCH else []) + [("a", c)]
+            fill = planes(c + 2, by_vector[c + 2]) if c + 2 < NCH else products
+            for n in range(len(weights)):
+                vector_q += [("il",) + weights[n], fill[n], ("q",) + weights[n]]
             if c + 2 < NCH:
-                vector_q += planes(c + 2, by_vector[c + 2])
-        vector_q += finish(last - 1) + finish(last)
-        tensor_q += [("mx", "a", last - 1), ("mx", "a", last), ("thT", last - 1), ("thT", last)]
+                vector_q += fill[len(weights):]
+            else:
+                products = products[len(weights):]
+        vector_q += products
+        tensor_q += [("thT", last - 3), ("mx", "a", last - 1), ("mx", "a", last), ("thT", last - 2), ("thT", last - 1), ("thT", last)]
 
         nc.vector.memset(warm_in[:], 0.0)
         nc.vector.memset(brows[:], 0.0)

@@ -296,9 +296,8 @@ def tile_quantuminspiredneuralcore_pa_kernel(tc, x, amp_w, amp_b, ph_w_bytes, ph
         for i in range(NI):
             load_x(i)
         load_bias()
-        load_amp(0)
         load_bytes(2, 4)
-        for c in range(1, NCH):
+        for c in range(NCH):
             load_amp(c)
 
         queues = (scalar_q, vector_q, tensor_q)

@@ -85,7 +85,8 @@ def tile_quantuminspiredneuralcore_pa_kernel(tc, x, amp_w, amp_b, ph_w_bytes, ph
 
         def load_x(i):
             x_sb[i] = keep.tile([P, K], BF16, name="x_sb_%d" % i)
-            nc.sync.dma_start(out=x_sb[i][:], in_=xf[i * P:(i + 1) * P, :])
+            for lo, hi in ([(0, K)] if i < NI - 1 else [(0, K // G), (K // G, K)]):
+                nc.sync.dma_start(out=x_sb[i][:, lo:hi], in_=xf[i * P:(i + 1) * P, lo:hi])
 
         def load_bias():
             nc.sync.dma_start(out=brows[0:NT, :], in_=amp_b.rearrange("(j p) -> j p", p=P))
@@ -126,17 +127,19 @@ def tile_quantuminspiredneuralcore_pa_kernel(tc, x, amp_w, amp_b, ph_w_bytes, ph
             nc.vector.quantize_mx(out=codes[(w, c)][:].bitcast(FP8X4), scales=scales[(w, c)][:],
                                   in_=grouped[(w, c)][:].rearrange("p m t -> p (m t)"))
 
-        def x_turn(on_scalar, i):
-            xt[i] = psum.tile([P, G, 2, P], F32, name="xt_%d" % i, tag=("zp", "za")[i % 2])
+        def x_turn(on_scalar, i, first=0, passes=G):
+            tag = "tpT" if first else ("zp", "za")[i % 2]
+            xt[(i, first)] = psum.tile([P, passes, 2, P], F32, name="xt_%d_%d" % (i, first), tag=tag)
             words = x_sb[i][:].bitcast(F32)
-            for g in range(G):
+            for n in range(passes):
+                g = first + n
                 for u in range(2):
-                    nc.tensor.transpose(xt[i][:, g, u, :], words[:, 256 * g + u:256 * (g + 1):2], ident_f[:])
+                    nc.tensor.transpose(xt[(i, first)][:, n, u, :], words[:, 256 * g + u:256 * (g + 1):2], ident_f[:])
 
-        def x_copy(on_scalar, i):
+        def x_copy(on_scalar, i, first=0, passes=G):
             h, q = divmod(i, 2)
-            dst = x_grouped[h][:].bitcast(F32)[:, :, q * P:(q + 1) * P, :]
-            src = xt[i][:].rearrange("p g u r -> p g r u")
+            dst = x_grouped[h][:].bitcast(F32)[:, first:first + passes, q * P:(q + 1) * P, :]
+            src = xt[(i, first)][:].rearrange("p g u r -> p g r u")
             if on_scalar:
                 nc.scalar.copy(out=dst, in_=src)
             else:
@@ -218,9 +221,9 @@ def tile_quantuminspiredneuralcore_pa_kernel(tc, x, amp_w, amp_b, ph_w_bytes, ph
             if kind == "q":
                 return [("il", s[1], j)]
             if kind == "xc":
-                return [("xT", j)]
+                return [("xT",) + s[1:]]
             if kind == "xq":
-                return [("xc", 2 * s[1]), ("xc", 2 * s[1] + 1)]
+                return [("xc", 0), ("xc", 1)] if s[1] == 0 else [("xc", 2), ("xc", NI - 1, s[2], 1)]
             if kind == "bias":
                 return [("bT",)]
             if kind == "mx":
@@ -258,10 +261,10 @@ def tile_quantuminspiredneuralcore_pa_kernel(tc, x, amp_w, amp_b, ph_w_bytes, ph
         def finish(j):
             return [("sq", j), ("pr", j)] if j in by_half else [("pr", j)] if j < last else [("pr", j, 0, HALF), ("pr", j, HALF, TOK)]
 
-        scalar_q = planes(0, by_scalar[0]) + [("xc", i) for i in range(NI)] + planes(2, by_scalar[2])
+        scalar_q = planes(0, by_scalar[0]) + [("xc", i) for i in range(NI - 1)] + [("xc", NI - 1, g, 1) for g in range(G)] + planes(2, by_scalar[2])
         vector_q = planes(0, by_vector[0]) + planes(1, by_vector[1][:-1]) + [("il", "p", 0)] + planes(1, by_vector[1][-1:]) + [("q", "p", 0)]
         vector_q += [("xq", h, g) for h in range(2) for g in range(G)] + [("bias",)]
-        tensor_q = [("warm", n) for n in range(3)] + [("xT", 0), ("warm", 3), ("xT", 1), ("warm", 4), ("xT", 2), ("xT", 3), ("bT",)] + [("warm", n) for n in range(5, 8)]
+        tensor_q = [("warm", n) for n in range(3)] + [("xT", 0), ("warm", 3), ("xT", 1), ("warm", 4), ("xT", 2), ("xT", 3, 0, 1), ("xT", 3, 1, 1), ("bT",)] + [("warm", n) for n in range(5, 8)]
         products = [s for j in range(NT) for s in finish(j)]
         for c in range(NCH):
             new_tiles = [2 * c, 2 * c + 1]

@@ -264,7 +264,10 @@ def tile_quantuminspiredneuralcore_pa_kernel(tc, x, amp_w, amp_b, ph_w_bytes, ph
         scalar_q = planes(0, by_scalar[0]) + [("xc", i) for i in range(NI - 1)] + [("xc", NI - 1, g, 1) for g in range(G)] + planes(2, by_scalar[2])
         vector_q = planes(0, by_vector[0]) + planes(1, by_vector[1][:-1]) + [("il", "p", 0)] + planes(1, by_vector[1][-1:]) + [("q", "p", 0)]
         vector_q += [("xq", h, g) for h in range(2) for g in range(G)] + [("bias",)]
-        tensor_q = [("warm", n) for n in range(3)] + [("xT", 0), ("warm", 3), ("xT", 1), ("warm", 4), ("xT", 2), ("xT", 3, 0, 1), ("xT", 3, 1, 1), ("bT",)] + [("warm", n) for n in range(5, 8)]
+        tensor_q = [("warm", n) for n in range(6)]
+        for i in range(NI - 1):
+            tensor_q += [("xT", i), ("warm", 6 + i)]
+        tensor_q += [("xT", NI - 1, 0, 1), ("xT", NI - 1, 1, 1), ("bT",)] + [("warm", n) for n in range(9, 12)]
         products = [s for j in range(NT) for s in finish(j)]
         for c in range(NCH):
             new_tiles = [2 * c, 2 * c + 1]

import math
from contextlib import ExitStack

import concourse.mybir as mybir
from concourse.masks import make_identity

FLOPS = 2 * 2 * 512 * 1024 * 1024

F32 = mybir.dt.float32
BF16 = mybir.dt.bfloat16
U32 = mybir.dt.uint32
U8 = mybir.dt.uint8
FP8 = mybir.dt.float8_e4m3fn
FP8X4 = mybir.dt.float8_e4m3fn_x4
ACT = mybir.ActivationFunctionType
ALU = mybir.AluOpType

P = 128
TOK = 512
K = 1024
N = 1024
G = 2
T = 4
NW = 256
NCH = N // NW
NT = N // P
TPC = NW // P
NI = TOK // P
HALF = TOK // 2
DEPTH = 5


def tile_quantuminspiredneuralcore_pa_kernel(tc, x, amp_w, amp_b, ph_w_bytes, ph_w_scale, ph_b, out):
    nc = tc.nc
    xf = x.flatten_outer_dims()
    of = out.flatten_outer_dims()
    amp_v = amp_w.rearrange("(g p t) n -> g p t n", p=P, t=T)
    phb_v = ph_w_bytes.rearrange("(g p t) n -> g p t n", p=P, t=T)
    phs_v = ph_w_scale.rearrange("(g p t) o -> p g (t o)", p=P, t=T)
    out_v = of.rearrange("(i p) n -> p i n", p=P)

    with ExitStack() as ctx:
        keep = ctx.enter_context(tc.tile_pool(name="keep", bufs=1))
        work = ctx.enter_context(tc.tile_pool(name="work", bufs=DEPTH))
        psum = ctx.enter_context(tc.psum_pool(name="psum", bufs=2))
        ctx.enter_context(tc.manual_schedule())

        warm_in = keep.tile([P, 1], F32, name="warm_in")
        warm_out = keep.tile([P, 1], F32, name="warm_out")
        brows = keep.tile([P, P], BF16, name="brows")
        ident_f = keep.tile([P, P], F32, name="ident_f")
        ident_b = keep.tile([P, P], BF16, name="ident_b")
        ones_b = keep.tile([P, TOK], BF16, name="ones_b")
        ph_scale = keep.tile([P, G, T], F32, name="ph_scale")
        bias = keep.tile([P, 2 * NT], F32, name="bias")
        x_grouped = [keep.tile([P, G, HALF, T], BF16, name="x_grouped_%d" % h, align_bytes=64) for h in range(2)]
        x_codes = keep.tile([P, G, TOK], U32, name="x_codes", align_bytes=64)
        x_scales = keep.tile([P, G, TOK], U8, name="x_scales", align_bytes=64)

        by_half = (5,)
        paired = (1, 3)
        ph_bytes = {}
        raw = {}
        x_sb = {}
        xt = {}
        grouped = {}
        codes = {}
        scales = {}
        acc = {}
        ep = {}

        def load_bytes(c0, c1, pieces=1):
            for g in range(G):
                both = keep.tile([P, T, (c1 - c0) * NW], U8, name="ph_bytes_%d_%d" % (c0, g))
                step = T // pieces
                for t0 in range(0, T, step):
                    nc.sync.dma_start(out=both[:, t0:t0 + step, :], in_=phb_v[g][:, t0:t0 + step, c0 * NW:c1 * NW])
                for c in range(c0, c1):
                    ph_bytes[(c, g)] = both[:, :, (c - c0) * NW:(c - c0 + 1) * NW]

        def load_amp(c):
            raw[("a", c)] = keep.tile([P, T, G, NW], BF16, name="amp_raw_%d" % c)
            for g in range(G):
                nc.sync.dma_start(out=raw[("a", c)][:, :, g, :], in_=amp_v[g][:, :, c * NW:(c + 1) * NW])

        def load_x(i):
            x_sb[i] = keep.tile([P, K], BF16, name="x_sb_%d" % i)
            for lo, hi in ([(0, K)] if i < NI - 1 else [(0, K // G), (K // G, K)]):
                nc.sync.dma_start(out=x_sb[i][:, lo:hi], in_=xf[i * P:(i + 1) * P, lo:hi])

        def load_bias():
            nc.sync.dma_start(out=brows[0:NT, :], in_=amp_b.rearrange("(j p) -> j p", p=P))
            nc.sync.dma_start(out=brows[NT:2 * NT, :], in_=ph_b.rearrange("(j p) -> j p", p=P))

        def bias_turn(on_scalar):
            ep["bT"] = psum.tile([P, P], BF16, name="bT", tag="tpT")
            nc.tensor.transpose(ep["bT"][:], brows[:], ident_b[:])

        def bias_copy(on_scalar):
            nc.vector.tensor_scalar(out=bias[:, 0:NT], in0=ep["bT"][:, 0:NT], scalar1=0.5, scalar2=None, op0=ALU.mult)
            nc.vector.tensor_copy(out=bias[:, NT:2 * NT], in_=ep["bT"][:, NT:2 * NT])

        def widen(on_scalar, c, k):
            if ("p", c) not in raw:
                shape = [P, 2, G, NW, 2] if c in paired else [P, T, G, NW]
                raw[("p", c)] = keep.tile(shape, BF16, name="ph_wide_%d" % c)
            g, t = divmod(k, T)
            src = ph_bytes[(c, g)][:, t, :].bitcast(FP8)
            dst = raw[("p", c)][:, t // 2, g, :, t % 2] if c in paired else raw[("p", c)][:, t, g, :]
            if on_scalar:
                nc.scalar.activation(out=dst, in_=src, func=ACT.Copy, scale=ph_scale[:, g, t:t + 1])
            else:
                nc.vector.tensor_scalar(out=dst, in0=src, scalar1=ph_scale[:, g, t:t + 1], scalar2=None, op0=ALU.mult)

        def interleave(on_scalar, w, c):
            grouped[(w, c)] = keep.tile([P, G * NW, T], BF16, name="grouped_%s_%d" % (w, c), align_bytes=64)
            if w == "p" and c in paired:
                nc.vector.tensor_copy(out=grouped[(w, c)][:].rearrange("p m (u e) -> p m u e", e=2),
                                      in_=raw[(w, c)][:].rearrange("p u g n e -> p u (g n) e").rearrange("p u m e -> p m u e"))
            else:
                nc.vector.tensor_copy(out=grouped[(w, c)][:].rearrange("p (c i) t -> p c t i", i=4),
                                      in_=raw[(w, c)][:].rearrange("p t g n -> p t (g n)").rearrange("p t (c i) -> p c t i", i=4))

        def quantize(on_scalar, w, c):
            codes[(w, c)] = keep.tile([P, G * NW], U32, name="codes_%s_%d" % (w, c), align_bytes=64)
            scales[(w, c)] = keep.tile([P, G * NW], U8, name="scales_%s_%d" % (w, c), align_bytes=64)
            nc.vector.quantize_mx(out=codes[(w, c)][:].bitcast(FP8X4), scales=scales[(w, c)][:],
                                  in_=grouped[(w, c)][:].rearrange("p m t -> p (m t)"))

        def x_turn(on_scalar, i, first=0, passes=G):
            tag = "tpT" if first else ("zp", "za")[i % 2]
            xt[(i, first)] = psum.tile([P, passes, 2, P], F32, name="xt_%d_%d" % (i, first), tag=tag)
            words = x_sb[i][:].bitcast(F32)
            for n in range(passes):
                g = first + n
                for u in range(2):
                    nc.tensor.transpose(xt[(i, first)][:, n, u, :], words[:, 256 * g + u:256 * (g + 1):2], ident_f[:])

        def x_copy(on_scalar, i, first=0, passes=G):
            h, q = divmod(i, 2)
            dst = x_grouped[h][:].bitcast(F32)[:, first:first + passes, q * P:(q + 1) * P, :]
            src = xt[(i, first)][:].rearrange("p g u r -> p g r u")
            if on_scalar:
                nc.scalar.copy(out=dst, in_=src)
            else:
                nc.vector.tensor_copy(out=dst, in_=src)

        def x_quantize(on_scalar, h, g):
            lo, hi = h * HALF, (h + 1) * HALF
            nc.vector.quantize_mx(out=x_codes[:, g, lo:hi].bitcast(FP8X4), scales=x_scales[:, g, lo:hi],
                                  in_=x_grouped[h][:, g].rearrange("p r t -> p (r t)"))

        def multiply(on_scalar, w, j):
            c, h = divmod(j, TPC)
            acc[(w, j)] = psum.tile([P, TOK], F32, name="acc_%s_%d" % (w, j), tag="z" + w)
            for g in range(G):
                cols = slice(g * NW + h * P, g * NW + (h + 1) * P)
                nc.tensor.matmul_mx(out=acc[(w, j)][:],
                                    lhsT=codes[(w, c)][:, cols].bitcast(FP8X4), lhsT_scale=scales[(w, c)][:, cols],
                                    rhs=x_codes[:, g, :].bitcast(FP8X4), rhs_scale=x_scales[:, g, :],
                                    start=(g == 0), stop=(g == G - 1))

        def new(kind, j):
            ep[(kind, j)] = work.tile([P, TOK], F32, name="%s_%d" % (kind, j), tag=kind)
            return ep[(kind, j)]

        def tanh_ph(on_scalar, j):
            nc.scalar.activation(out=new("tp", j)[:], in_=acc[("p", j)][:], func=ACT.Tanh, bias=bias[:, NT + j:NT + j + 1], scale=1.0)

        def tanh_amp(on_scalar, j):
            nc.scalar.activation(out=new("th", j)[:], in_=acc[("a", j)][:], func=ACT.Tanh, bias=bias[:, j:j + 1], scale=0.5)

        def turn_ph(on_scalar, j):
            ep[("tpT", j)] = psum.tile([P, TOK], F32, name="tpT_%d" % j, tag="tpT")
            for i in range(NI):
                nc.tensor.transpose(ep[("tpT", j)][:, i * P:(i + 1) * P], ep[("tp", j)][:, i * P:(i + 1) * P], ident_f[:])

        def turn_amp(on_scalar, j):
            ep[("thT", j)] = psum.tile([P, TOK], F32, name="thT_%d" % j, tag="thT" if j < NT - TPC else "tpT")
            nc.tensor.matmul(out=ep[("thT", j)][:], lhsT=ident_b[:], rhs=ones_b[:], start=True, stop=False)
            for i in range(NI):
                nc.tensor.matmul(out=ep[("thT", j)][:, i * P:(i + 1) * P], lhsT=ep[("th", j)][:, i * P:(i + 1) * P], rhs=ident_f[:],
                                 is_transpose=True, start=False, stop=(i == NI - 1))

        def fold(on_scalar, j):
            nc.scalar.activation(out=new("ab", j)[:], in_=ep[("tpT", j)][:], func=ACT.Abs, bias=-0.25, scale=1.0)

        def half_sine(on_scalar, j):
            nc.scalar.activation(out=new("sn", j)[:], in_=ep[("tpT", j)][:], func=ACT.Sin, bias=-math.pi / 8, scale=math.pi / 2)

        def square(on_scalar, j):
            nc.vector.scalar_tensor_tensor(out=new("sq", j)[:], in0=ep[("sn", j)][:], scalar=-math.sqrt(2.0), in1=ep[("sn", j)][:],
                                           op0=ALU.mult, op1=ALU.mult)

        def sine(on_scalar, j, lo=0, hi=TOK):
            if lo == 0:
                new("sn", j)
            nc.scalar.activation(out=ep[("sn", j)][:, lo:hi], in_=ep[("ab", j)][:, lo:hi], func=ACT.Sin, bias=math.pi / 2, scale=-math.pi)

        def product(on_scalar, j, lo=0, hi=TOK):
            o_sb = work.tile([P, hi - lo], F32, name="o_sb_%d_%d" % (j, lo), tag="o_sb", bufs=4)
            kind, first = ("sq", ALU.add) if j in by_half else ("sn", ALU.mult)
            nc.vector.scalar_tensor_tensor(out=o_sb[:], in0=ep[(kind, j)][:, lo:hi], scalar=math.sqrt(0.5),
                                           in1=ep[("thT", j)][:, lo:hi], op0=first, op1=ALU.mult)
            nc.sync.dma_start(out=out_v[:, lo // P:hi // P, j * P:(j + 1) * P], in_=o_sb[:].rearrange("p (i n) -> p i n", n=P))

        def warm_up(on_scalar, n):
            dummy = psum.tile([P, TOK], F32, name="dummy_%d" % n, tag="thT")
            nc.tensor.matmul(out=dummy[:, 0:P], lhsT=ident_f[:], rhs=ident_f[:], start=True, stop=True)

        steps = {"warm": warm_up, "bT": bias_turn, "bias": bias_copy, "widen": widen, "il": interleave, "q": quantize, "xT": x_turn, "xc": x_copy,
                 "xq": x_quantize, "mx": multiply, "tp": tanh_ph, "th": tanh_amp, "tpT": turn_ph, "thT": turn_amp, "ab": fold,
                 "hs": half_sine, "sq": square, "sn": sine, "pr": product}

        def needs(s):
            kind = s[0]
            j = s[2] if kind in ("il", "q", "mx") else s[-1] if len(s) == 2 else s[1] if len(s) > 1 else 0
            x_done = [("xq", h, g) for h in range(2) for g in range(G)]
            if kind == "il":
                return [("widen", j, k) for k in range(G * T)] if s[1] == "p" else []
            if kind == "q":
                return [("il", s[1], j)]
            if kind == "xc":
                return [("xT",) + s[1:]]
            if kind == "xq":
                return [("xc", 0), ("xc", 1)] if s[1] == 0 else [("xc", 2), ("xc", NI - 1, s[2], 1)]
            if kind == "bias":
                return [("bT",)]
            if kind == "mx":
                return [("q", s[1], j // TPC)] + x_done + ([({"p": "tp", "a": "th"}[s[1]], j - 2)] if j >= 2 else [])
            if kind == "tp":
                return [("mx", "p", j), ("bias",)] + ([("tpT", j - DEPTH)] if j >= DEPTH else [])
            if kind == "th":
                return [("mx", "a", j), ("bias",)] + ([("thT", j - DEPTH)] if j >= DEPTH else [])
            if kind == "tpT":
                return [("tp", j), ("bias",)] + ([fold_of(j - 2)] if j >= 2 else [])
            if kind == "thT":
                return [("th", j)] + ([fold_of(j)] if j >= NT - TPC else [("pr", j - 2)] if j >= 2 else [])
            if kind == "ab":
                return [("tpT", j)] + ([("sn", j - DEPTH)] if j >= DEPTH and j - DEPTH not in by_half else [])
            if kind == "sn":
                return [("ab", j)] + ([("pr", j - DEPTH + 1)] if j >= DEPTH - 1 else [])
            if kind == "hs":
                return [("tpT", j)] + ([("pr", j - DEPTH + 1)] if j >= DEPTH - 1 else [])
            if kind == "sq":
                return [("hs", j)]
            if kind == "pr":
                return [("sq", j) if j in by_half else ("sn",) + s[1:], ("thT", j)]
            return []

        def fold_of(j):
            return ("hs", j) if j in by_half else ("ab", j)

        def planes(c, ks):
            return [("widen", c, k) for k in ks]

        last = NT - 1
        by_scalar = {0: (2, 3, 4, 5, 6, 7), 1: (), 2: (2, 3, 4, 5, 6, 7), 3: ()}
        by_vector = {c: tuple(k for k in (0, 2, 1, 3, 4, 6, 5, 7) if k not in by_scalar[c]) for c in range(NCH)}

        def finish(j):
            return [("sq", j), ("pr", j)] if j in by_half else [("pr", j)] if j < last else [("pr", j, 0, HALF), ("pr", j, HALF, TOK)]

        scalar_q = planes(0, by_scalar[0]) + [("xc", i) for i in range(NI - 1)] + [("xc", NI - 1, g, 1) for g in range(G)] + planes(2, by_scalar[2])
        vector_q = planes(0, by_vector[0]) + planes(1, by_vector[1][:-1]) + [("il", "p", 0)] + planes(1, by_vector[1][-1:]) + [("q", "p", 0)]
        vector_q += [("xq", h, g) for h in range(2) for g in range(G)] + [("bias",)]
        tensor_q = [("warm", n) for n in range(6)]
        for i in range(NI - 1):
            tensor_q += [("xT", i), ("warm", 6 + i)]
        tensor_q += [("xT", NI - 1, 0, 1), ("xT", NI - 1, 1, 1), ("bT",)] + [("warm", n) for n in range(9, 12)]
        products = [s for j in range(NT) for s in finish(j)]
        for c in range(NCH):
            new_tiles = [2 * c, 2 * c + 1]
            old_tiles = [2 * c - 2, 2 * c - 1] if c else []
            tensor_q += [("mx", "p", j) for j in new_tiles]
            tensor_q += [("thT", j - 2) for j in old_tiles if j >= 2]
            tensor_q += [("mx", "a", j) for j in old_tiles] + [("tpT", j) for j in new_tiles]
            scalar_q += [("tp", j) for j in new_tiles] + [("th", j) for j in old_tiles]
            scalar_q += [fold_of(j) for j in new_tiles]
            for j in new_tiles:
                scalar_q += [] if j in by_half else [("sn", j)] if j < last else [("th", last - 1), ("th", last), ("sn", j, 0, HALF), ("sn", j, HALF, TOK)]
            weights = ([("p", c + 1)] if c + 1 < NCH else []) + [("a", c)]
            fill = planes(c + 2, by_vector[c + 2]) if c + 2 < NCH else products
            for n in range(len(weights)):
                vector_q += [("il",) + weights[n], fill[n], ("q",) + weights[n]]
            if c + 2 < NCH:
                vector_q += fill[len(weights):]
            else:
                products = products[len(weights):]
        vector_q += products
        tensor_q += [("thT", last - 3), ("mx", "a", last - 1), ("mx", "a", last), ("thT", last - 2), ("thT", last - 1), ("thT", last)]

        nc.vector.memset(warm_in[:], 0.0)
        nc.vector.memset(brows[:], 0.0)
        nc.vector.memset(ones_b[:], 1.0)
        nc.scalar.activation(out=warm_out[:], in_=warm_in[:], func=ACT.Silu)
        make_identity(nc, ident_f[:])
        make_identity(nc, ident_b[:])

        nc.sync.dma_start(out=ph_scale[:], in_=phs_v)
        load_bytes(0, 2)
        for i in range(NI):
            load_x(i)
        load_bias()
        load_bytes(2, 4)
        for c in range(NCH):
            load_amp(c)

        queues = (scalar_q, vector_q, tensor_q)
        heads = [0, 0, 0]
        written = set()
        while sum(heads) < sum(len(q) for q in queues):
            before = sum(heads)
            for e in range(3):
                while heads[e] < len(queues[e]) and all(n in written for n in needs(queues[e][heads[e]])):
                    s = queues[e][heads[e]]
                    steps[s[0]](e == 0, *s[1:])
                    written.add(s)
                    heads[e] += 1
            assert sum(heads) > before, "the queues wait for each other"
